import numpy as np
import ml_dtypes


def mxq(x, axis, fmt="e4m3"):
    dtype, down = {"e4m3": (ml_dtypes.float8_e4m3fn, 7), "e5m2": (ml_dtypes.float8_e5m2, 14)}[fmt]
    v = np.moveaxis(np.asarray(x, np.float32).astype(ml_dtypes.bfloat16).astype(np.float64), axis, -1)
    blocks = v.reshape(v.shape[:-1] + (-1, 32))
    amax = np.abs(blocks).max(-1, keepdims=True)
    byte = np.maximum(np.where(amax > 0, np.frexp(amax)[1] - 1 + 127, 0) - down, 1)
    scale = np.exp2(byte - 127.0)
    codes = (blocks / scale).astype(np.float32).astype(dtype).astype(np.float64)
    return np.moveaxis((codes * scale).reshape(v.shape), -1, axis)


WIDE = False


def mx_kscale(k):
    if not WIDE:
        return np.ones(k)
    levels = np.array([10, -10, 5, -5, 0])
    a = np.random.permutation(np.resize(levels, k // 512 * 4)).reshape(k // 512, 4)
    idx = np.arange(k)
    return np.exp2(a[idx // 512, idx % 128 // 32])


BF16 = ml_dtypes.bfloat16


def bf(x):
    return np.asarray(x, np.float32).astype(BF16)


def f64(x):
    return np.asarray(x).astype(np.float64)


B, C, S1, S2, S3, S4, S5 = 8, 512, 64, 32, 16, 8, 4
EPS = 1e-5
OFF = 0.5
SPAN = 9.0


def dynconv1x1(x, f):
    b, c, h, w = x.shape
    xq = mxq(x.reshape(b, c, h * w), 1, "e4m3")
    fq = mxq(f[..., 0, 0], 2, "e4m3")
    return (fq @ xq).reshape(b, f.shape[1], h, w)


def instance_norm(y):
    mu = y.mean(axis=(2, 3), keepdims=True)
    var = np.square(y - mu).mean(axis=(2, 3), keepdims=True)
    return (y - mu) / np.sqrt(var + EPS)


def draw_x(side, s):
    v = np.random.standard_normal((B, C, side, side)) + OFF * np.random.standard_normal((B, C, 1, 1))
    return bf(v * s[None, :, None, None])


def draw_f(s, span):
    g = np.exp2(-span * np.random.random((B, C, 1, 1, 1)))
    return bf(np.random.standard_normal((B, C, C, 1, 1)) / np.sqrt(C) * g / s[None, None, :, None, None])


def setup_inputs():
    s = mx_kscale(C)
    return {"x2": draw_x(S2, s), "l2fs": draw_f(s, SPAN)}


def reference(x2, l2fs):
    return instance_norm(dynconv1x1(f64(x2), f64(l2fs)))

@@ -1,0 +1,274 @@
+from contextlib import ExitStack
+
+import concourse.mybir as mybir
+from concourse.masks import make_identity
+
+F32 = mybir.dt.float32
+BF16 = mybir.dt.bfloat16
+U32 = mybir.dt.uint32
+U8 = mybir.dt.uint8
+FP8X4 = mybir.dt.float8_e4m3fn_x4
+ACT = mybir.ActivationFunctionType
+ALU = mybir.AluOpType
+
+NB = 8
+CH = 512
+POS = 1024
+P = 128
+NT = 4
+BANK = 512
+EPS = 1e-5
+FLOPS = 2 * NB * CH * CH * POS
+CV = 608
+CV0 = 336
+
+
+def tile_lingunet5filter_pa_kernel(tc, x2, l2fs, out):
+    nc = tc.nc
+    xv = x2.rearrange("b (u p e) h w -> b p u (e h w)", u=2, e=2)
+    xh = x2.rearrange("b (u p e) h w -> b u p e (h w)", u=2, e=2)
+    fv = l2fs.rearrange("b (p t) k x y -> b p (t k x y)", t=NT)
+    ov = out.rearrange("b (p t) h w -> b p t (h w)", t=NT)
+
+    with ExitStack() as ctx:
+        const = ctx.enter_context(tc.tile_pool(name="const", bufs=1))
+        raw = ctx.enter_context(tc.tile_pool(name="raw", bufs=NB))
+        grp = ctx.enter_context(tc.tile_pool(name="grp", bufs=3))
+        mxp = ctx.enter_context(tc.tile_pool(name="mxp", bufs=2))
+        outp = ctx.enter_context(tc.tile_pool(name="outp", bufs=8))
+        small = ctx.enter_context(tc.tile_pool(name="small", bufs=8))
+        psum = ctx.enter_context(tc.psum_pool(name="psum", bufs=8))
+
+        ident = const.tile([P, P], F32, name="ident")
+        make_identity(nc, ident[:])
+        mhalf = const.tile([P, 1], F32, name="mhalf")
+        nc.vector.memset(mhalf[:], -0.5)
+        warm = const.tile([P, 1], F32, name="warm")
+        nc.scalar.activation(out=warm[:], in_=mhalf[:], func=ACT.Identity)
+
+        ctx.enter_context(tc.manual_schedule())
+
+        xraw = {}
+        fraw = {}
+        xg = {}
+        fg = {}
+        ft = {}
+        xq = {}
+        fq = {}
+        ys = {}
+        mvs = {}
+        aff = {}
+        osb = {}
+
+        def load_x(b):
+            xraw[b] = raw.tile([P, 4, POS], BF16, name="xraw")
+            nc.sync.dma_start(
+                out=xraw[b][:].rearrange("p (u e) w -> p u (e w)", u=2), in_=xv[b]
+            )
+
+        def load_x_half(b, h):
+            if b not in xraw:
+                xraw[b] = raw.tile([P, 4, POS], BF16, name="xraw")
+            for u in range(2):
+                nc.sync.dma_start(
+                    out=xraw[b][:, 2 * u : 2 * u + 2, h * BANK : (h + 1) * BANK],
+                    in_=xh[b][u][:, :, h * BANK : (h + 1) * BANK],
+                )
+
+        def load_f(b):
+            fraw[b] = raw.tile([P, NT * CH], BF16, name="fraw")
+            nc.sync.dma_start(out=fraw[b][:], in_=fv[b])
+
+        def transposes(b):
+            fw = fraw[b][:].bitcast(F32)
+            for j in range(2):
+                ft[(b, j)] = psum.tile([P, 2, 2, P], F32, name="ft", tag="bank")
+                for tt in range(2):
+                    for u in range(2):
+                        c0 = (2 * j + tt) * 256 + u * P
+                        nc.tensor.transpose(
+                            ft[(b, j)][:, tt, u, :], fw[:, c0 : c0 + P], ident[:]
+                        )
+
+        def fcopy(copy, b, j):
+            if b not in fg:
+                fg[b] = grp.tile([P, 4 * CH], BF16, name="fg", align_bytes=64)
+            fgw = fg[b][:].bitcast(F32).rearrange(
+                "p (j tt o u) -> p j tt o u", j=2, tt=2, u=2
+            )
+            copy(out=fgw[:, j], in_=ft[(b, j)][:].rearrange("p tt u o -> p tt o u"))
+
+        def regroup(copy, b, c0, c1):
+            if b not in xg:
+                xg[b] = grp.tile([P, 4 * POS], BF16, name="xg", align_bytes=64)
+            copy(
+                out=xg[b][:, 4 * c0 : 4 * c1].rearrange(
+                    "p (c i t) -> p c t i", i=4, t=4
+                ),
+                in_=xraw[b][:, :, c0:c1].rearrange("p t (c i) -> p c t i", i=4),
+            )
+
+        def quant_f(b):
+            codes = mxp.tile([P, CH], U32, name="fc", align_bytes=64)
+            scales = mxp.tile([P, CH], U8, name="fs", align_bytes=64)
+            nc.vector.quantize_mx(
+                out=codes[:].bitcast(FP8X4), scales=scales[:], in_=fg[b][:]
+            )
+            fq[b] = (codes, scales)
+
+        def quant_x(b, c0, c1):
+            if b not in xq:
+                codes = mxp.tile([P, POS], U32, name="xc", align_bytes=64)
+                scales = mxp.tile([P, POS], U8, name="xs", align_bytes=64)
+                xq[b] = (codes, scales)
+            codes, scales = xq[b]
+            nc.vector.quantize_mx(
+                out=codes[:, c0:c1].bitcast(FP8X4),
+                scales=scales[:, c0:c1],
+                in_=xg[b][:, 4 * c0 : 4 * c1],
+            )
+
+        def mm(b, t):
+            fc, fs = fq[b]
+            xc, xs = xq[b]
+            for n in range(2):
+                y = psum.tile([P, BANK], F32, name="y", tag="bank")
+                nc.tensor.matmul_mx(
+                    out=y[:],
+                    lhsT=fc[:, t * P : (t + 1) * P].bitcast(FP8X4),
+                    lhsT_scale=fs[:, t * P : (t + 1) * P],
+                    rhs=xc[:, n * BANK : (n + 1) * BANK].bitcast(FP8X4),
+                    rhs_scale=xs[:, n * BANK : (n + 1) * BANK],
+                    start=True,
+                    stop=True,
+                )
+                ys[(b, t, n)] = y
+
+        def stats(b, t):
+            st = small.tile([P, 2, 6], F32, name="st")
+            for n in range(2):
+                nc.vector.bn_stats(out=st[:, n, :], in_=ys[(b, t, n)][:])
+            mv = small.tile([P, 2], F32, name="mv")
+            nc.vector.bn_aggr(out=mv[:], in_=st[:].rearrange("p n s -> p (n s)"))
+            mvs[(b, t)] = mv
+
+        def affine(b, t):
+            mv = mvs[(b, t)]
+            ve = small.tile([P, 1], F32, name="ve")
+            nc.gpsimd.tensor_scalar(
+                out=ve[:], in0=mv[:, 1:2], scalar1=1.0, scalar2=EPS,
+                op0=ALU.mult, op1=ALU.add,
+            )
+            rstd = small.tile([P, 1], F32, name="rstd")
+            nc.gpsimd.tensor_tensor(out=rstd[:], in0=ve[:], in1=mhalf[:], op=ALU.pow)
+            nbias = small.tile([P, 1], F32, name="nbias")
+            nc.gpsimd.tensor_scalar(
+                out=nbias[:], in0=mv[:, 0:1], scalar1=rstd[:], scalar2=-1.0,
+                op0=ALU.mult, op1=ALU.mult,
+            )
+            aff[(b, t)] = (rstd, nbias)
+
+        def norm(b, t):
+            rstd, nbias = aff[(b, t)]
+            if t % 2 == 0:
+                osb[b] = outp.tile([P, 2, POS], F32, name="osb")
+            for n in range(2):
+                nc.scalar.activation(
+                    out=osb[b][:, t % 2, n * BANK : (n + 1) * BANK],
+                    in_=ys[(b, t, n)][:],
+                    func=ACT.Identity,
+                    bias=nbias[:],
+                    scale=rstd[:],
+                )
+
+        vcopy = nc.vector.tensor_copy
+        scopy = nc.scalar.copy
+        half_v = CV // 2
+        half_s = (CV + POS) // 2
+
+        first = -4
+        last = NB * NT
+        pe_after = {}
+        v_after = {}
+        s_after = {}
+        for s in range(first, last):
+            pe_after[s] = []
+            v_after[s] = []
+            s_after[s] = []
+        for k in range(1, NB):
+            base = NT * k
+            s_after[base - 8].append(("rs", k, CV, half_s))
+            s_after[base - 7].append(("rs", k, half_s, POS))
+            v_after[base - 5].append(("rv", k, 0, half_v))
+            v_after[base - 4].append(("rv", k, half_v, CV))
+            if k == 1:
+                pe_after[-1].append(k)
+                s_after[0].append(("c", k, 0))
+                s_after[0].append(("c", k, 1))
+                v_after[2].append(("qx", k))
+                v_after[2].append(("qf", k))
+            else:
+                pe_after[base - 7].append(k)
+                s_after[base - 6].append(("c", k, 0))
+                s_after[base - 5].append(("c", k, 1))
+                v_after[base - 3].append(("qf", k))
+                v_after[base - 2].append(("qx", k))
+
+        def extras(s):
+            for a in s_after[s]:
+                if a[0] == "rs":
+                    regroup(scopy, a[1], a[2], a[3])
+                else:
+                    fcopy(scopy, a[1], a[2])
+            for a in v_after[s]:
+                if a[0] == "rv":
+                    regroup(vcopy, a[1], a[2], a[3])
+                elif a[0] == "qf":
+                    quant_f(a[1])
+                else:
+                    quant_x(a[1], 0, POS)
+
+        load_x_half(0, 0)
+        load_f(0)
+        load_x_half(0, 1)
+        for b in range(1, 5):
+            load_x(b)
+            load_f(b)
+
+        regroup(vcopy, 0, 0, CV0)
+        regroup(scopy, 0, CV0, BANK)
+        transposes(0)
+        quant_x(0, 0, BANK)
+        fcopy(scopy, 0, 0)
+        fcopy(vcopy, 0, 1)
+        regroup(vcopy, 0, BANK, BANK + CV0)
+        regroup(scopy, 0, BANK + CV0, POS)
+        quant_f(0)
+        quant_x(0, BANK, POS)
+        mm(0, 0)
+        mm(0, 1)
+        for s in range(first, 0):
+            extras(s)
+            for k in pe_after[s]:
+                transposes(k)
+
+        for s in range(last):
+            b = s // NT
+            t = s % NT
+            stats(b, t)
+            affine(b, t)
+            norm(b, t)
+            if b == NB - 1:
+                nc.sync.dma_start(
+                    out=ov[b][:, t : t + 1, :], in_=osb[b][:, t % 2 : t % 2 + 1, :]
+                )
+            elif t % 2 == 1:
+                nc.sync.dma_start(out=ov[b][:, t - 1 : t + 1, :], in_=osb[b][:])
+            extras(s)
+            if s + 2 < last:
+                mm((s + 2) // NT, (s + 2) % NT)
+            for k in pe_after[s]:
+                transposes(k)
+            if t == NT - 1 and b + 5 < NB:
+                load_x(b + 5)
+                load_f(b + 5)

@@ -21,6 +21,7 @@ EPS = 1e-5
 FLOPS = 2 * NB * CH * CH * POS
 CV = 608
 CV0 = 336
+VTAIL = 2
 
 
 def tile_lingunet5filter_pa_kernel(tc, x2, l2fs, out):
@@ -34,10 +35,11 @@ def tile_lingunet5filter_pa_kernel(tc, x2, l2fs, out):
         const = ctx.enter_context(tc.tile_pool(name="const", bufs=1))
         raw = ctx.enter_context(tc.tile_pool(name="raw", bufs=NB))
         grp = ctx.enter_context(tc.tile_pool(name="grp", bufs=3))
-        mxp = ctx.enter_context(tc.tile_pool(name="mxp", bufs=2))
+        mxp = ctx.enter_context(tc.tile_pool(name="mxp", bufs=3))
         outp = ctx.enter_context(tc.tile_pool(name="outp", bufs=8))
         small = ctx.enter_context(tc.tile_pool(name="small", bufs=8))
-        psum = ctx.enter_context(tc.psum_pool(name="psum", bufs=8))
+        pv = ctx.enter_context(tc.psum_pool(name="pv", bufs=4))
+        ps = ctx.enter_context(tc.psum_pool(name="ps", bufs=4))
 
         ident = const.tile([P, P], F32, name="ident")
         make_identity(nc, ident[:])
@@ -56,6 +58,7 @@ def tile_lingunet5filter_pa_kernel(tc, x2, l2fs, out):
         xq = {}
         fq = {}
         ys = {}
+        yn = {}
         mvs = {}
         aff = {}
         osb = {}
@@ -82,7 +85,7 @@ def tile_lingunet5filter_pa_kernel(tc, x2, l2fs, out):
         def transposes(b):
             fw = fraw[b][:].bitcast(F32)
             for j in range(2):
-                ft[(b, j)] = psum.tile([P, 2, 2, P], F32, name="ft", tag="bank")
+                ft[(b, j)] = ps.tile([P, 2, 2, P], F32, name="ft", tag="sbank")
                 for tt in range(2):
                     for u in range(2):
                         c0 = (2 * j + tt) * 256 + u * P
@@ -128,11 +131,11 @@ def tile_lingunet5filter_pa_kernel(tc, x2, l2fs, out):
                 in_=xg[b][:, 4 * c0 : 4 * c1],
             )
 
-        def mm(b, t):
+        def mm(pool, tag, keep, b, t):
             fc, fs = fq[b]
             xc, xs = xq[b]
             for n in range(2):
-                y = psum.tile([P, BANK], F32, name="y", tag="bank")
+                y = pool.tile([P, BANK], F32, name=tag)
                 nc.tensor.matmul_mx(
                     out=y[:],
                     lhsT=fc[:, t * P : (t + 1) * P].bitcast(FP8X4),
@@ -142,7 +145,7 @@ def tile_lingunet5filter_pa_kernel(tc, x2, l2fs, out):
                     start=True,
                     stop=True,
                 )
-                ys[(b, t, n)] = y
+                keep[(b, t, n)] = y
 
         def stats(b, t):
             st = small.tile([P, 2, 6], F32, name="st")
@@ -173,20 +176,25 @@ def tile_lingunet5filter_pa_kernel(tc, x2, l2fs, out):
             if t % 2 == 0:
                 osb[b] = outp.tile([P, 2, POS], F32, name="osb")
             for n in range(2):
-                nc.scalar.activation(
-                    out=osb[b][:, t % 2, n * BANK : (n + 1) * BANK],
-                    in_=ys[(b, t, n)][:],
-                    func=ACT.Identity,
-                    bias=nbias[:],
-                    scale=rstd[:],
-                )
+                dst = osb[b][:, t % 2, n * BANK : (n + 1) * BANK]
+                if n == 1 and NT * b + t >= NB * NT - VTAIL:
+                    nc.vector.tensor_scalar(
+                        out=dst, in0=yn[(b, t, n)][:],
+                        scalar1=mvs[(b, t)][:, 0:1], scalar2=rstd[:],
+                        op0=ALU.subtract, op1=ALU.mult,
+                    )
+                else:
+                    nc.scalar.activation(
+                        out=dst, in_=yn[(b, t, n)][:], func=ACT.Identity,
+                        bias=nbias[:], scale=rstd[:],
+                    )
 
         vcopy = nc.vector.tensor_copy
         scopy = nc.scalar.copy
         half_v = CV // 2
         half_s = (CV + POS) // 2
 
-        first = -4
+        first = -5
         last = NB * NT
         pe_after = {}
         v_after = {}
@@ -197,29 +205,24 @@ def tile_lingunet5filter_pa_kernel(tc, x2, l2fs, out):
             s_after[s] = []
         for k in range(1, NB):
             base = NT * k
-            s_after[base - 8].append(("rs", k, CV, half_s))
-            s_after[base - 7].append(("rs", k, half_s, POS))
+            s_after[base - 9].append(("rs", k, CV, half_s))
+            s_after[base - 8].append(("rs", k, half_s, POS))
+            pe_after[base - 7].append(k)
+            s_after[base - 7].append(("c", k, 0))
+            s_after[base - 7].append(("c", k, 1))
             v_after[base - 5].append(("rv", k, 0, half_v))
             v_after[base - 4].append(("rv", k, half_v, CV))
-            if k == 1:
-                pe_after[-1].append(k)
-                s_after[0].append(("c", k, 0))
-                s_after[0].append(("c", k, 1))
-                v_after[2].append(("qx", k))
-                v_after[2].append(("qf", k))
-            else:
-                pe_after[base - 7].append(k)
-                s_after[base - 6].append(("c", k, 0))
-                s_after[base - 5].append(("c", k, 1))
-                v_after[base - 3].append(("qf", k))
-                v_after[base - 2].append(("qx", k))
+            v_after[base - 3].append(("qf", k))
+            v_after[base - 2].append(("qx", k))
 
-        def extras(s):
+        def s_extras(s):
             for a in s_after[s]:
                 if a[0] == "rs":
                     regroup(scopy, a[1], a[2], a[3])
                 else:
                     fcopy(scopy, a[1], a[2])
+
+        def v_extras(s):
             for a in v_after[s]:
                 if a[0] == "rv":
                     regroup(vcopy, a[1], a[2], a[3])
@@ -231,7 +234,7 @@ def tile_lingunet5filter_pa_kernel(tc, x2, l2fs, out):
         load_x_half(0, 0)
         load_f(0)
         load_x_half(0, 1)
-        for b in range(1, 5):
+        for b in range(1, NB):
             load_x(b)
             load_f(b)
 
@@ -245,30 +248,33 @@ def tile_lingunet5filter_pa_kernel(tc, x2, l2fs, out):
         regroup(scopy, 0, BANK + CV0, POS)
         quant_f(0)
         quant_x(0, BANK, POS)
-        mm(0, 0)
-        mm(0, 1)
+        mm(pv, "yv", ys, 0, 0)
+        mm(pv, "yv", ys, 0, 1)
         for s in range(first, 0):
-            extras(s)
             for k in pe_after[s]:
                 transposes(k)
+            s_extras(s)
+            v_extras(s)
 
-        for s in range(last):
-            b = s // NT
-            t = s % NT
-            stats(b, t)
-            affine(b, t)
-            norm(b, t)
-            if b == NB - 1:
-                nc.sync.dma_start(
-                    out=ov[b][:, t : t + 1, :], in_=osb[b][:, t % 2 : t % 2 + 1, :]
-                )
-            elif t % 2 == 1:
-                nc.sync.dma_start(out=ov[b][:, t - 1 : t + 1, :], in_=osb[b][:])
-            extras(s)
-            if s + 2 < last:
-                mm((s + 2) // NT, (s + 2) % NT)
-            for k in pe_after[s]:
-                transposes(k)
-            if t == NT - 1 and b + 5 < NB:
-                load_x(b + 5)
-                load_f(b + 5)
+        for step in range(last + 1):
+            if step < last:
+                stats(step // NT, step % NT)
+                affine(step // NT, step % NT)
+                v_extras(step)
+                if step + 2 < last:
+                    mm(pv, "yv", ys, (step + 2) // NT, (step + 2) % NT)
+            s = step - 1
+            if s >= 0:
+                b = s // NT
+                t = s % NT
+                mm(ps, "sbank", yn, b, t)
+                for k in pe_after[s]:
+                    transposes(k)
+                norm(b, t)
+                if b == NB - 1:
+                    nc.sync.dma_start(
+                        out=ov[b][:, t : t + 1, :], in_=osb[b][:, t % 2 : t % 2 + 1, :]
+                    )
+                elif t % 2 == 1:
+                    nc.sync.dma_start(out=ov[b][:, t - 1 : t + 1, :], in_=osb[b][:])
+                s_extras(s)

@@ -19,7 +19,7 @@ NT = 4
 BANK = 512
 EPS = 1e-5
 FLOPS = 2 * NB * CH * CH * POS
-CV = 608
+CV = 448
 CV0 = 336
 VTAIL = 2
 

@@ -19,9 +19,12 @@ NT = 4
 BANK = 512
 EPS = 1e-5
 FLOPS = 2 * NB * CH * CH * POS
-CV = 448
+CVB = 128
 CV0 = 336
+GPIECE = 256
 VTAIL = 2
+FINE = 5
+LAG = 2
 
 
 def tile_lingunet5filter_pa_kernel(tc, x2, l2fs, out):
@@ -34,6 +37,7 @@ def tile_lingunet5filter_pa_kernel(tc, x2, l2fs, out):
     with ExitStack() as ctx:
         const = ctx.enter_context(tc.tile_pool(name="const", bufs=1))
         raw = ctx.enter_context(tc.tile_pool(name="raw", bufs=NB))
+        gone = ctx.enter_context(tc.tile_pool(name="gone", bufs=1))
         grp = ctx.enter_context(tc.tile_pool(name="grp", bufs=3))
         mxp = ctx.enter_context(tc.tile_pool(name="mxp", bufs=3))
         outp = ctx.enter_context(tc.tile_pool(name="outp", bufs=8))
@@ -43,9 +47,9 @@ def tile_lingunet5filter_pa_kernel(tc, x2, l2fs, out):
 
         ident = const.tile([P, P], F32, name="ident")
         make_identity(nc, ident[:])
-        mhalf = const.tile([P, 1], F32, name="mhalf")
+        mhalf = const.tile([P, 2], F32, name="mhalf")
         nc.vector.memset(mhalf[:], -0.5)
-        warm = const.tile([P, 1], F32, name="warm")
+        warm = const.tile([P, 2], F32, name="warm")
         nc.scalar.activation(out=warm[:], in_=mhalf[:], func=ACT.Identity)
 
         ctx.enter_context(tc.manual_schedule())
@@ -93,23 +97,43 @@ def tile_lingunet5filter_pa_kernel(tc, x2, l2fs, out):
                             ft[(b, j)][:, tt, u, :], fw[:, c0 : c0 + P], ident[:]
                         )
 
-        def fcopy(copy, b, j):
+        def fcopy(b, j):
             if b not in fg:
                 fg[b] = grp.tile([P, 4 * CH], BF16, name="fg", align_bytes=64)
             fgw = fg[b][:].bitcast(F32).rearrange(
                 "p (j tt o u) -> p j tt o u", j=2, tt=2, u=2
             )
-            copy(out=fgw[:, j], in_=ft[(b, j)][:].rearrange("p tt u o -> p tt o u"))
+            nc.scalar.copy(
+                out=fgw[:, j], in_=ft[(b, j)][:].rearrange("p tt u o -> p tt o u")
+            )
 
-        def regroup(copy, b, c0, c1):
-            if b not in xg:
-                xg[b] = grp.tile([P, 4 * POS], BF16, name="xg", align_bytes=64)
+        def grouped(b, h):
+            if (b, h) not in xg:
+                if h == 0:
+                    xg[(b, h)] = gone.tile([P, 4 * BANK], BF16, name="xga", align_bytes=64)
+                else:
+                    xg[(b, h)] = grp.tile([P, 4 * BANK], BF16, name="xgb", align_bytes=64)
+            return xg[(b, h)]
+
+        def regroup(copy, b, h, c0, c1):
             copy(
-                out=xg[b][:, 4 * c0 : 4 * c1].rearrange(
+                out=grouped(b, h)[:, 4 * c0 : 4 * c1].rearrange(
                     "p (c i t) -> p c t i", i=4, t=4
                 ),
-                in_=xraw[b][:, :, c0:c1].rearrange("p t (c i) -> p c t i", i=4),
+                in_=xraw[b][:, :, h * BANK + c0 : h * BANK + c1].rearrange(
+                    "p t (c i) -> p c t i", i=4
+                ),
             )
+
+        def regroup_g(b):
+            for c0 in range(0, BANK, GPIECE):
+                nc.gpsimd.tensor_scalar(
+                    out=grouped(b, 0)[:, 4 * c0 : 4 * (c0 + GPIECE)].rearrange(
+                        "p (c t) -> p c t", t=4
+                    ),
+                    in0=xraw[b][:, :, c0 : c0 + GPIECE].rearrange("p t c -> p c t"),
+                    scalar1=1.0, scalar2=0.0, op0=ALU.mult, op1=ALU.add,
+                )
 
         def quant_f(b):
             codes = mxp.tile([P, CH], U32, name="fc", align_bytes=64)
@@ -119,19 +143,21 @@ def tile_lingunet5filter_pa_kernel(tc, x2, l2fs, out):
             )
             fq[b] = (codes, scales)
 
-        def quant_x(b, c0, c1):
+        def quant_x(b, h):
             if b not in xq:
                 codes = mxp.tile([P, POS], U32, name="xc", align_bytes=64)
                 scales = mxp.tile([P, POS], U8, name="xs", align_bytes=64)
                 xq[b] = (codes, scales)
             codes, scales = xq[b]
             nc.vector.quantize_mx(
-                out=codes[:, c0:c1].bitcast(FP8X4),
-                scales=scales[:, c0:c1],
-                in_=xg[b][:, 4 * c0 : 4 * c1],
+                out=codes[:, h * BANK : (h + 1) * BANK].bitcast(FP8X4),
+                scales=scales[:, h * BANK : (h + 1) * BANK],
+                in_=xg[(b, h)][:],
             )
 
-        def mm(pool, tag, keep, b, t):
+        def mm(pool, tag, keep, s):
+            b = s // NT
+            t = s % NT
             fc, fs = fq[b]
             xc, xs = xq[b]
             for n in range(2):
@@ -145,136 +171,126 @@ def tile_lingunet5filter_pa_kernel(tc, x2, l2fs, out):
                     start=True,
                     stop=True,
                 )
-                keep[(b, t, n)] = y
+                keep[(s, n)] = y
 
-        def stats(b, t):
-            st = small.tile([P, 2, 6], F32, name="st")
-            for n in range(2):
-                nc.vector.bn_stats(out=st[:, n, :], in_=ys[(b, t, n)][:])
-            mv = small.tile([P, 2], F32, name="mv")
-            nc.vector.bn_aggr(out=mv[:], in_=st[:].rearrange("p n s -> p (n s)"))
-            mvs[(b, t)] = mv
+        def stats_pair(s):
+            st = small.tile([P, 2, 2, 6], F32, name="st")
+            for i in range(2):
+                for n in range(2):
+                    nc.vector.bn_stats(out=st[:, i, n, :], in_=ys[(s + i, n)][:])
+            mv = small.tile([P, 2, 2], F32, name="mv")
+            for i in range(2):
+                nc.vector.bn_aggr(
+                    out=mv[:, i, :], in_=st[:, i].rearrange("p n s -> p (n s)")
+                )
+            mvs[s] = mv
 
-        def affine(b, t):
-            mv = mvs[(b, t)]
-            ve = small.tile([P, 1], F32, name="ve")
+        def affine_pair(s):
+            mv = mvs[s]
+            negmu = small.tile([P, 2], F32, name="negmu")
+            nc.vector.tensor_scalar(
+                out=negmu[:], in0=mv[:, :, 0], scalar1=-1.0, scalar2=None, op0=ALU.mult
+            )
+            ve = small.tile([P, 2], F32, name="ve")
             nc.gpsimd.tensor_scalar(
-                out=ve[:], in0=mv[:, 1:2], scalar1=1.0, scalar2=EPS,
+                out=ve[:], in0=mv[:, :, 1], scalar1=1.0, scalar2=EPS,
                 op0=ALU.mult, op1=ALU.add,
             )
-            rstd = small.tile([P, 1], F32, name="rstd")
+            rstd = small.tile([P, 2], F32, name="rstd")
             nc.gpsimd.tensor_tensor(out=rstd[:], in0=ve[:], in1=mhalf[:], op=ALU.pow)
-            nbias = small.tile([P, 1], F32, name="nbias")
-            nc.gpsimd.tensor_scalar(
-                out=nbias[:], in0=mv[:, 0:1], scalar1=rstd[:], scalar2=-1.0,
-                op0=ALU.mult, op1=ALU.mult,
-            )
-            aff[(b, t)] = (rstd, nbias)
+            nbias = small.tile([P, 2], F32, name="nbias")
+            nc.gpsimd.tensor_tensor(out=nbias[:], in0=negmu[:], in1=rstd[:], op=ALU.mult)
+            aff[s] = (rstd, nbias)
 
-        def norm(b, t):
-            rstd, nbias = aff[(b, t)]
-            if t % 2 == 0:
-                osb[b] = outp.tile([P, 2, POS], F32, name="osb")
+        def norm(s):
+            i = s % 2
+            rstd, nbias = aff[s - i]
+            if i == 0:
+                osb[s // 2] = outp.tile([P, 2, POS], F32, name="osb")
             for n in range(2):
-                dst = osb[b][:, t % 2, n * BANK : (n + 1) * BANK]
-                if n == 1 and NT * b + t >= NB * NT - VTAIL:
+                dst = osb[s // 2][:, i, n * BANK : (n + 1) * BANK]
+                if n == 1 and s >= NB * NT - VTAIL:
                     nc.vector.tensor_scalar(
-                        out=dst, in0=yn[(b, t, n)][:],
-                        scalar1=mvs[(b, t)][:, 0:1], scalar2=rstd[:],
+                        out=dst, in0=yn[(s, n)][:],
+                        scalar1=mvs[s - i][:, i, 0:1], scalar2=rstd[:, i : i + 1],
                         op0=ALU.subtract, op1=ALU.mult,
                     )
                 else:
                     nc.scalar.activation(
-                        out=dst, in_=yn[(b, t, n)][:], func=ACT.Identity,
-                        bias=nbias[:], scale=rstd[:],
+                        out=dst, in_=yn[(s, n)][:], func=ACT.Identity,
+                        bias=nbias[:, i : i + 1], scale=rstd[:, i : i + 1],
                     )
+
+        def store(s):
+            b = s // NT
+            t = s % NT
+            if b >= FINE:
+                nc.sync.dma_start(
+                    out=ov[b][:, t : t + 1, :], in_=osb[s // 2][:, t % 2 : t % 2 + 1, :]
+                )
+            elif t % 2 == 1:
+                nc.sync.dma_start(out=ov[b][:, t - 1 : t + 1, :], in_=osb[s // 2][:])
 
         vcopy = nc.vector.tensor_copy
         scopy = nc.scalar.copy
-        half_v = CV // 2
-        half_s = (CV + POS) // 2
-
-        first = -5
+        mid_s = (CVB + BANK) // 2
         last = NB * NT
-        pe_after = {}
-        v_after = {}
-        s_after = {}
-        for s in range(first, last):
-            pe_after[s] = []
-            v_after[s] = []
-            s_after[s] = []
-        for k in range(1, NB):
-            base = NT * k
-            s_after[base - 9].append(("rs", k, CV, half_s))
-            s_after[base - 8].append(("rs", k, half_s, POS))
-            pe_after[base - 7].append(k)
-            s_after[base - 7].append(("c", k, 0))
-            s_after[base - 7].append(("c", k, 1))
-            v_after[base - 5].append(("rv", k, 0, half_v))
-            v_after[base - 4].append(("rv", k, half_v, CV))
-            v_after[base - 3].append(("qf", k))
-            v_after[base - 2].append(("qx", k))
 
-        def s_extras(s):
-            for a in s_after[s]:
-                if a[0] == "rs":
-                    regroup(scopy, a[1], a[2], a[3])
-                else:
-                    fcopy(scopy, a[1], a[2])
+        def s_prep(k):
+            regroup(scopy, k, 1, CVB, mid_s)
+            regroup(scopy, k, 1, mid_s, BANK)
+            fcopy(k, 0)
+            fcopy(k, 1)
 
-        def v_extras(s):
-            for a in v_after[s]:
-                if a[0] == "rv":
-                    regroup(vcopy, a[1], a[2], a[3])
-                elif a[0] == "qf":
-                    quant_f(a[1])
-                else:
-                    quant_x(a[1], 0, POS)
+        def quant_run(k):
+            regroup(vcopy, k, 1, 0, CVB)
+            quant_f(k)
+            quant_x(k, 0)
+            quant_x(k, 1)
+            if k + 1 < NB:
+                regroup_g(k + 1)
 
-        load_x_half(0, 0)
         load_f(0)
+        load_x_half(0, 0)
         load_x_half(0, 1)
         for b in range(1, NB):
             load_x(b)
             load_f(b)
 
-        regroup(vcopy, 0, 0, CV0)
-        regroup(scopy, 0, CV0, BANK)
         transposes(0)
-        quant_x(0, 0, BANK)
-        fcopy(scopy, 0, 0)
-        fcopy(vcopy, 0, 1)
-        regroup(vcopy, 0, BANK, BANK + CV0)
-        regroup(scopy, 0, BANK + CV0, POS)
+        fcopy(0, 0)
+        fcopy(0, 1)
+        regroup(vcopy, 0, 0, 0, CV0)
+        regroup(scopy, 0, 0, CV0, BANK)
         quant_f(0)
-        quant_x(0, BANK, POS)
-        mm(pv, "yv", ys, 0, 0)
-        mm(pv, "yv", ys, 0, 1)
-        for s in range(first, 0):
-            for k in pe_after[s]:
-                transposes(k)
-            s_extras(s)
-            v_extras(s)
+        quant_x(0, 0)
+        regroup(vcopy, 0, 1, 0, CV0)
+        regroup(scopy, 0, 1, CV0, BANK)
+        quant_x(0, 1)
+        regroup_g(1)
+        mm(pv, "yv", ys, 0)
+        mm(pv, "yv", ys, 1)
+        transposes(1)
+        s_prep(1)
 
-        for step in range(last + 1):
+        for step in range(last + LAG):
             if step < last:
-                stats(step // NT, step % NT)
-                affine(step // NT, step % NT)
-                v_extras(step)
+                if step % 2 == 0:
+                    stats_pair(step)
+                    if step % NT == 0 and step // NT + 1 < NB:
+                        quant_run(step // NT + 1)
+                    affine_pair(step)
                 if step + 2 < last:
-                    mm(pv, "yv", ys, (step + 2) // NT, (step + 2) % NT)
-            s = step - 1
+                    mm(pv, "yv", ys, step + 2)
+            s = step - LAG
             if s >= 0:
-                b = s // NT
-                t = s % NT
-                mm(ps, "sbank", yn, b, t)
-                for k in pe_after[s]:
-                    transposes(k)
-                norm(b, t)
-                if b == NB - 1:
-                    nc.sync.dma_start(
-                        out=ov[b][:, t : t + 1, :], in_=osb[b][:, t % 2 : t % 2 + 1, :]
-                    )
-                elif t % 2 == 1:
-                    nc.sync.dma_start(out=ov[b][:, t - 1 : t + 1, :], in_=osb[b][:])
-                s_extras(s)
+                mm(ps, "sbank", yn, s)
+            k = (s + 9) // NT
+            prep = (s + 9) % NT == 0 and 2 <= k < NB
+            if prep:
+                transposes(k)
+            if s >= 0:
+                norm(s)
+                store(s)
+            if prep:
+                s_prep(k)

@@ -19,9 +19,8 @@ NT = 4
 BANK = 512
 EPS = 1e-5
 FLOPS = 2 * NB * CH * CH * POS
-CVB = 128
+CV = 448
 CV0 = 336
-GPIECE = 256
 VTAIL = 2
 FINE = 5
 LAG = 2
@@ -37,7 +36,6 @@ def tile_lingunet5filter_pa_kernel(tc, x2, l2fs, out):
     with ExitStack() as ctx:
         const = ctx.enter_context(tc.tile_pool(name="const", bufs=1))
         raw = ctx.enter_context(tc.tile_pool(name="raw", bufs=NB))
-        gone = ctx.enter_context(tc.tile_pool(name="gone", bufs=1))
         grp = ctx.enter_context(tc.tile_pool(name="grp", bufs=3))
         mxp = ctx.enter_context(tc.tile_pool(name="mxp", bufs=3))
         outp = ctx.enter_context(tc.tile_pool(name="outp", bufs=8))
@@ -107,33 +105,15 @@ def tile_lingunet5filter_pa_kernel(tc, x2, l2fs, out):
                 out=fgw[:, j], in_=ft[(b, j)][:].rearrange("p tt u o -> p tt o u")
             )
 
-        def grouped(b, h):
-            if (b, h) not in xg:
-                if h == 0:
-                    xg[(b, h)] = gone.tile([P, 4 * BANK], BF16, name="xga", align_bytes=64)
-                else:
-                    xg[(b, h)] = grp.tile([P, 4 * BANK], BF16, name="xgb", align_bytes=64)
-            return xg[(b, h)]
-
-        def regroup(copy, b, h, c0, c1):
+        def regroup(copy, b, c0, c1):
+            if b not in xg:
+                xg[b] = grp.tile([P, 4 * POS], BF16, name="xg", align_bytes=64)
             copy(
-                out=grouped(b, h)[:, 4 * c0 : 4 * c1].rearrange(
+                out=xg[b][:, 4 * c0 : 4 * c1].rearrange(
                     "p (c i t) -> p c t i", i=4, t=4
                 ),
-                in_=xraw[b][:, :, h * BANK + c0 : h * BANK + c1].rearrange(
-                    "p t (c i) -> p c t i", i=4
-                ),
+                in_=xraw[b][:, :, c0:c1].rearrange("p t (c i) -> p c t i", i=4),
             )
-
-        def regroup_g(b):
-            for c0 in range(0, BANK, GPIECE):
-                nc.gpsimd.tensor_scalar(
-                    out=grouped(b, 0)[:, 4 * c0 : 4 * (c0 + GPIECE)].rearrange(
-                        "p (c t) -> p c t", t=4
-                    ),
-                    in0=xraw[b][:, :, c0 : c0 + GPIECE].rearrange("p t c -> p c t"),
-                    scalar1=1.0, scalar2=0.0, op0=ALU.mult, op1=ALU.add,
-                )
 
         def quant_f(b):
             codes = mxp.tile([P, CH], U32, name="fc", align_bytes=64)
@@ -143,16 +123,16 @@ def tile_lingunet5filter_pa_kernel(tc, x2, l2fs, out):
             )
             fq[b] = (codes, scales)
 
-        def quant_x(b, h):
+        def quant_x(b, c0, c1):
             if b not in xq:
                 codes = mxp.tile([P, POS], U32, name="xc", align_bytes=64)
                 scales = mxp.tile([P, POS], U8, name="xs", align_bytes=64)
                 xq[b] = (codes, scales)
             codes, scales = xq[b]
             nc.vector.quantize_mx(
-                out=codes[:, h * BANK : (h + 1) * BANK].bitcast(FP8X4),
-                scales=scales[:, h * BANK : (h + 1) * BANK],
-                in_=xg[(b, h)][:],
+                out=codes[:, c0:c1].bitcast(FP8X4),
+                scales=scales[:, c0:c1],
+                in_=xg[b][:, 4 * c0 : 4 * c1],
             )
 
         def mm(pool, tag, keep, s):
@@ -233,22 +213,21 @@ def tile_lingunet5filter_pa_kernel(tc, x2, l2fs, out):
 
         vcopy = nc.vector.tensor_copy
         scopy = nc.scalar.copy
-        mid_s = (CVB + BANK) // 2
+        mid_s = (CV + POS) // 2
         last = NB * NT
 
         def s_prep(k):
-            regroup(scopy, k, 1, CVB, mid_s)
-            regroup(scopy, k, 1, mid_s, BANK)
+            regroup(scopy, k, CV, mid_s)
+            regroup(scopy, k, mid_s, POS)
             fcopy(k, 0)
             fcopy(k, 1)
 
+        def v_prep(k):
+            regroup(vcopy, k, 0, CV)
+
         def quant_run(k):
-            regroup(vcopy, k, 1, 0, CVB)
             quant_f(k)
-            quant_x(k, 0)
-            quant_x(k, 1)
-            if k + 1 < NB:
-                regroup_g(k + 1)
+            quant_x(k, 0, POS)
 
         load_f(0)
         load_x_half(0, 0)
@@ -260,16 +239,16 @@ def tile_lingunet5filter_pa_kernel(tc, x2, l2fs, out):
         transposes(0)
         fcopy(0, 0)
         fcopy(0, 1)
-        regroup(vcopy, 0, 0, 0, CV0)
-        regroup(scopy, 0, 0, CV0, BANK)
+        regroup(vcopy, 0, 0, CV0)
+        regroup(scopy, 0, CV0, BANK)
         quant_f(0)
-        quant_x(0, 0)
-        regroup(vcopy, 0, 1, 0, CV0)
-        regroup(scopy, 0, 1, CV0, BANK)
-        quant_x(0, 1)
-        regroup_g(1)
+        quant_x(0, 0, BANK)
+        regroup(vcopy, 0, BANK, BANK + CV0)
+        regroup(scopy, 0, BANK + CV0, POS)
+        quant_x(0, BANK, POS)
         mm(pv, "yv", ys, 0)
         mm(pv, "yv", ys, 1)
+        v_prep(1)
         transposes(1)
         s_prep(1)
 
@@ -280,6 +259,8 @@ def tile_lingunet5filter_pa_kernel(tc, x2, l2fs, out):
                     if step % NT == 0 and step // NT + 1 < NB:
                         quant_run(step // NT + 1)
                     affine_pair(step)
+                    if step % NT == 2 and (step + 6) // NT < NB:
+                        v_prep((step + 6) // NT)
                 if step + 2 < last:
                     mm(pv, "yv", ys, step + 2)
             s = step - LAG

@@ -19,6 +19,7 @@ NT = 4
 BANK = 512
 EPS = 1e-5
 FLOPS = 2 * NB * CH * CH * POS
+CG = 256
 CV = 448
 CV0 = 336
 VTAIL = 2
@@ -36,6 +37,7 @@ def tile_lingunet5filter_pa_kernel(tc, x2, l2fs, out):
     with ExitStack() as ctx:
         const = ctx.enter_context(tc.tile_pool(name="const", bufs=1))
         raw = ctx.enter_context(tc.tile_pool(name="raw", bufs=NB))
+        gone = ctx.enter_context(tc.tile_pool(name="gone", bufs=1))
         grp = ctx.enter_context(tc.tile_pool(name="grp", bufs=3))
         mxp = ctx.enter_context(tc.tile_pool(name="mxp", bufs=3))
         outp = ctx.enter_context(tc.tile_pool(name="outp", bufs=8))
@@ -105,14 +107,26 @@ def tile_lingunet5filter_pa_kernel(tc, x2, l2fs, out):
                 out=fgw[:, j], in_=ft[(b, j)][:].rearrange("p tt u o -> p tt o u")
             )
 
+        def grouped(b, c0, c1):
+            if c1 <= CG:
+                if (b, 0) not in xg:
+                    xg[(b, 0)] = gone.tile([P, 4 * CG], BF16, name="xga", align_bytes=64)
+                return xg[(b, 0)][:, 4 * c0 : 4 * c1]
+            if (b, 1) not in xg:
+                xg[(b, 1)] = grp.tile([P, 4 * (POS - CG)], BF16, name="xgb", align_bytes=64)
+            return xg[(b, 1)][:, 4 * (c0 - CG) : 4 * (c1 - CG)]
+
         def regroup(copy, b, c0, c1):
-            if b not in xg:
-                xg[b] = grp.tile([P, 4 * POS], BF16, name="xg", align_bytes=64)
             copy(
-                out=xg[b][:, 4 * c0 : 4 * c1].rearrange(
-                    "p (c i t) -> p c t i", i=4, t=4
-                ),
+                out=grouped(b, c0, c1).rearrange("p (c i t) -> p c t i", i=4, t=4),
                 in_=xraw[b][:, :, c0:c1].rearrange("p t (c i) -> p c t i", i=4),
+            )
+
+        def regroup_g(b):
+            nc.gpsimd.tensor_scalar(
+                out=grouped(b, 0, CG).rearrange("p (c t) -> p c t", t=4),
+                in0=xraw[b][:, :, 0:CG].rearrange("p t c -> p c t"),
+                scalar1=1.0, scalar2=0.0, op0=ALU.mult, op1=ALU.add,
             )
 
         def quant_f(b):
@@ -132,7 +146,7 @@ def tile_lingunet5filter_pa_kernel(tc, x2, l2fs, out):
             nc.vector.quantize_mx(
                 out=codes[:, c0:c1].bitcast(FP8X4),
                 scales=scales[:, c0:c1],
-                in_=xg[b][:, 4 * c0 : 4 * c1],
+                in_=grouped(b, c0, c1),
             )
 
         def mm(pool, tag, keep, s):
@@ -223,11 +237,15 @@ def tile_lingunet5filter_pa_kernel(tc, x2, l2fs, out):
             fcopy(k, 1)
 
         def v_prep(k):
-            regroup(vcopy, k, 0, CV)
+            regroup(vcopy, k, CG, CV)
 
         def quant_run(k):
             quant_f(k)
-            quant_x(k, 0, POS)
+            quant_x(k, 0, CG)
+            quant_x(k, CG, BANK)
+            quant_x(k, BANK, POS)
+            if k + 1 < NB:
+                regroup_g(k + 1)
 
         load_f(0)
         load_x_half(0, 0)
@@ -239,13 +257,16 @@ def tile_lingunet5filter_pa_kernel(tc, x2, l2fs, out):
         transposes(0)
         fcopy(0, 0)
         fcopy(0, 1)
-        regroup(vcopy, 0, 0, CV0)
+        regroup(vcopy, 0, 0, CG)
+        regroup(vcopy, 0, CG, CV0)
         regroup(scopy, 0, CV0, BANK)
         quant_f(0)
-        quant_x(0, 0, BANK)
+        quant_x(0, 0, CG)
+        quant_x(0, CG, BANK)
         regroup(vcopy, 0, BANK, BANK + CV0)
         regroup(scopy, 0, BANK + CV0, POS)
         quant_x(0, BANK, POS)
+        regroup_g(1)
         mm(pv, "yv", ys, 0)
         mm(pv, "yv", ys, 1)
         v_prep(1)

@@ -19,8 +19,8 @@ NT = 4
 BANK = 512
 EPS = 1e-5
 FLOPS = 2 * NB * CH * CH * POS
-CG = 256
-CV = 448
+CG = 512
+CV = 640
 CV0 = 336
 VTAIL = 2
 FINE = 5
@@ -37,7 +37,6 @@ def tile_lingunet5filter_pa_kernel(tc, x2, l2fs, out):
     with ExitStack() as ctx:
         const = ctx.enter_context(tc.tile_pool(name="const", bufs=1))
         raw = ctx.enter_context(tc.tile_pool(name="raw", bufs=NB))
-        gone = ctx.enter_context(tc.tile_pool(name="gone", bufs=1))
         grp = ctx.enter_context(tc.tile_pool(name="grp", bufs=3))
         mxp = ctx.enter_context(tc.tile_pool(name="mxp", bufs=3))
         outp = ctx.enter_context(tc.tile_pool(name="outp", bufs=8))
@@ -86,16 +85,15 @@ def tile_lingunet5filter_pa_kernel(tc, x2, l2fs, out):
             fraw[b] = raw.tile([P, NT * CH], BF16, name="fraw")
             nc.sync.dma_start(out=fraw[b][:], in_=fv[b])
 
-        def transposes(b):
+        def transposes(b, j):
             fw = fraw[b][:].bitcast(F32)
-            for j in range(2):
-                ft[(b, j)] = ps.tile([P, 2, 2, P], F32, name="ft", tag="sbank")
-                for tt in range(2):
-                    for u in range(2):
-                        c0 = (2 * j + tt) * 256 + u * P
-                        nc.tensor.transpose(
-                            ft[(b, j)][:, tt, u, :], fw[:, c0 : c0 + P], ident[:]
-                        )
+            ft[(b, j)] = ps.tile([P, 2, 2, P], F32, name="ft", tag="sbank")
+            for tt in range(2):
+                for u in range(2):
+                    c0 = (2 * j + tt) * 256 + u * P
+                    nc.tensor.transpose(
+                        ft[(b, j)][:, tt, u, :], fw[:, c0 : c0 + P], ident[:]
+                    )
 
         def fcopy(b, j):
             if b not in fg:
@@ -108,13 +106,9 @@ def tile_lingunet5filter_pa_kernel(tc, x2, l2fs, out):
             )
 
         def grouped(b, c0, c1):
-            if c1 <= CG:
-                if (b, 0) not in xg:
-                    xg[(b, 0)] = gone.tile([P, 4 * CG], BF16, name="xga", align_bytes=64)
-                return xg[(b, 0)][:, 4 * c0 : 4 * c1]
-            if (b, 1) not in xg:
-                xg[(b, 1)] = grp.tile([P, 4 * (POS - CG)], BF16, name="xgb", align_bytes=64)
-            return xg[(b, 1)][:, 4 * (c0 - CG) : 4 * (c1 - CG)]
+            if b not in xg:
+                xg[b] = grp.tile([P, 4 * POS], BF16, name="xg", align_bytes=64)
+            return xg[b][:, 4 * c0 : 4 * c1]
 
         def regroup(copy, b, c0, c1):
             copy(
@@ -122,10 +116,10 @@ def tile_lingunet5filter_pa_kernel(tc, x2, l2fs, out):
                 in_=xraw[b][:, :, c0:c1].rearrange("p t (c i) -> p c t i", i=4),
             )
 
-        def regroup_g(b):
+        def regroup_g(b, c0, c1):
             nc.gpsimd.tensor_scalar(
-                out=grouped(b, 0, CG).rearrange("p (c t) -> p c t", t=4),
-                in0=xraw[b][:, :, 0:CG].rearrange("p t c -> p c t"),
+                out=grouped(b, c0, c1).rearrange("p (c t) -> p c t", t=4),
+                in0=xraw[b][:, :, c0:c1].rearrange("p t c -> p c t"),
                 scalar1=1.0, scalar2=0.0, op0=ALU.mult, op1=ALU.add,
             )
 
@@ -181,10 +175,6 @@ def tile_lingunet5filter_pa_kernel(tc, x2, l2fs, out):
 
         def affine_pair(s):
             mv = mvs[s]
-            negmu = small.tile([P, 2], F32, name="negmu")
-            nc.vector.tensor_scalar(
-                out=negmu[:], in0=mv[:, :, 0], scalar1=-1.0, scalar2=None, op0=ALU.mult
-            )
             ve = small.tile([P, 2], F32, name="ve")
             nc.gpsimd.tensor_scalar(
                 out=ve[:], in0=mv[:, :, 1], scalar1=1.0, scalar2=EPS,
@@ -192,6 +182,11 @@ def tile_lingunet5filter_pa_kernel(tc, x2, l2fs, out):
             )
             rstd = small.tile([P, 2], F32, name="rstd")
             nc.gpsimd.tensor_tensor(out=rstd[:], in0=ve[:], in1=mhalf[:], op=ALU.pow)
+            negmu = small.tile([P, 2], F32, name="negmu")
+            nc.gpsimd.tensor_scalar(
+                out=negmu[:], in0=mv[:, :, 0], scalar1=-1.0, scalar2=0.0,
+                op0=ALU.mult, op1=ALU.add,
+            )
             nbias = small.tile([P, 2], F32, name="nbias")
             nc.gpsimd.tensor_tensor(out=nbias[:], in0=negmu[:], in1=rstd[:], op=ALU.mult)
             aff[s] = (rstd, nbias)
@@ -230,48 +225,54 @@ def tile_lingunet5filter_pa_kernel(tc, x2, l2fs, out):
         mid_s = (CV + POS) // 2
         last = NB * NT
 
-        def s_prep(k):
-            regroup(scopy, k, CV, mid_s)
-            regroup(scopy, k, mid_s, POS)
-            fcopy(k, 0)
-            fcopy(k, 1)
+        def s_piece(k, j):
+            regroup(scopy, k, (CV, mid_s)[j], (mid_s, POS)[j])
 
         def v_prep(k):
             regroup(vcopy, k, CG, CV)
 
+        def g_piece(r):
+            k = r // 2
+            j = r % 2
+            regroup_g(k, j * CG // 2, (j + 1) * CG // 2)
+
         def quant_run(k):
             quant_f(k)
-            quant_x(k, 0, CG)
-            quant_x(k, CG, BANK)
-            quant_x(k, BANK, POS)
-            if k + 1 < NB:
-                regroup_g(k + 1)
+            quant_x(k, 0, POS)
 
         load_f(0)
         load_x_half(0, 0)
         load_x_half(0, 1)
         for b in range(1, NB):
-            load_x(b)
             load_f(b)
+            load_x(b)
 
-        transposes(0)
+        for b in range(2):
+            for j in range(2):
+                transposes(b, j)
         fcopy(0, 0)
         fcopy(0, 1)
-        regroup(vcopy, 0, 0, CG)
-        regroup(vcopy, 0, CG, CV0)
+        regroup(vcopy, 0, 0, CV0)
         regroup(scopy, 0, CV0, BANK)
         quant_f(0)
-        quant_x(0, 0, CG)
-        quant_x(0, CG, BANK)
+        quant_x(0, 0, BANK)
         regroup(vcopy, 0, BANK, BANK + CV0)
         regroup(scopy, 0, BANK + CV0, POS)
         quant_x(0, BANK, POS)
-        regroup_g(1)
+        g_piece(2)
+        g_piece(3)
         mm(pv, "yv", ys, 0)
         mm(pv, "yv", ys, 1)
         v_prep(1)
-        transposes(1)
-        s_prep(1)
+        for k in range(1, 3):
+            if k == 2:
+                for j in range(2):
+                    transposes(k, j)
+            for j in range(2):
+                fcopy(k, j)
+            for j in range(2):
+                s_piece(k, j)
+        g_piece(4)
 
         for step in range(last + LAG):
             if step < last:
@@ -280,19 +281,25 @@ def tile_lingunet5filter_pa_kernel(tc, x2, l2fs, out):
                     if step % NT == 0 and step // NT + 1 < NB:
                         quant_run(step // NT + 1)
                     affine_pair(step)
+                    r = step // 2 + 5
+                    if r // 2 < NB:
+                        g_piece(r)
                     if step % NT == 2 and (step + 6) // NT < NB:
                         v_prep((step + 6) // NT)
-                if step + 2 < last:
-                    mm(pv, "yv", ys, step + 2)
             s = step - LAG
             if s >= 0:
+                k = s // NT + 3
+                slot = s % NT
                 mm(ps, "sbank", yn, s)
-            k = (s + 9) // NT
-            prep = (s + 9) % NT == 0 and 2 <= k < NB
-            if prep:
-                transposes(k)
+                if k < NB and slot % 2 == 0:
+                    transposes(k, slot // 2)
+            if step + 2 < last:
+                mm(pv, "yv", ys, step + 2)
             if s >= 0:
                 norm(s)
                 store(s)
-            if prep:
-                s_prep(k)
+                if k < NB:
+                    if slot % 2 == 0:
+                        fcopy(k, slot // 2)
+                    else:
+                        s_piece(k, slot // 2)

@@ -20,11 +20,12 @@ BANK = 512
 EPS = 1e-5
 FLOPS = 2 * NB * CH * CH * POS
 CG = 512
-CV = 640
+CV = 704
 CV0 = 336
 VTAIL = 2
 FINE = 5
-LAG = 2
+LAG = 3
+LAG_P = 2
 
 
 def tile_lingunet5filter_pa_kernel(tc, x2, l2fs, out):
@@ -37,6 +38,7 @@ def tile_lingunet5filter_pa_kernel(tc, x2, l2fs, out):
     with ExitStack() as ctx:
         const = ctx.enter_context(tc.tile_pool(name="const", bufs=1))
         raw = ctx.enter_context(tc.tile_pool(name="raw", bufs=NB))
+        gone = ctx.enter_context(tc.tile_pool(name="gone", bufs=1))
         grp = ctx.enter_context(tc.tile_pool(name="grp", bufs=3))
         mxp = ctx.enter_context(tc.tile_pool(name="mxp", bufs=3))
         outp = ctx.enter_context(tc.tile_pool(name="outp", bufs=8))
@@ -48,8 +50,13 @@ def tile_lingunet5filter_pa_kernel(tc, x2, l2fs, out):
         make_identity(nc, ident[:])
         mhalf = const.tile([P, 2], F32, name="mhalf")
         nc.vector.memset(mhalf[:], -0.5)
+        epst = const.tile([P, 1], F32, name="epst")
+        nc.vector.tensor_scalar(
+            out=epst[:], in0=mhalf[:, 0:1], scalar1=0.0, scalar2=EPS,
+            op0=ALU.mult, op1=ALU.add,
+        )
         warm = const.tile([P, 2], F32, name="warm")
-        nc.scalar.activation(out=warm[:], in_=mhalf[:], func=ACT.Identity)
+        nc.scalar.activation(out=warm[:], in_=mhalf[:], func=ACT.Abs_reciprocal_sqrt)
 
         ctx.enter_context(tc.manual_schedule())
 
@@ -62,6 +69,7 @@ def tile_lingunet5filter_pa_kernel(tc, x2, l2fs, out):
         fq = {}
         ys = {}
         yn = {}
+        sts = {}
         mvs = {}
         aff = {}
         osb = {}
@@ -106,9 +114,13 @@ def tile_lingunet5filter_pa_kernel(tc, x2, l2fs, out):
             )
 
         def grouped(b, c0, c1):
-            if b not in xg:
-                xg[b] = grp.tile([P, 4 * POS], BF16, name="xg", align_bytes=64)
-            return xg[b][:, 4 * c0 : 4 * c1]
+            if c1 <= CG:
+                if (b, 0) not in xg:
+                    xg[(b, 0)] = gone.tile([P, 4 * CG], BF16, name="xga", align_bytes=64)
+                return xg[(b, 0)][:, 4 * c0 : 4 * c1]
+            if (b, 1) not in xg:
+                xg[(b, 1)] = grp.tile([P, 4 * (POS - CG)], BF16, name="xgb", align_bytes=64)
+            return xg[(b, 1)][:, 4 * (c0 - CG) : 4 * (c1 - CG)]
 
         def regroup(copy, b, c0, c1):
             copy(
@@ -161,34 +173,48 @@ def tile_lingunet5filter_pa_kernel(tc, x2, l2fs, out):
                 )
                 keep[(s, n)] = y
 
-        def stats_pair(s):
-            st = small.tile([P, 2, 2, 6], F32, name="st")
-            for i in range(2):
-                for n in range(2):
-                    nc.vector.bn_stats(out=st[:, i, n, :], in_=ys[(s + i, n)][:])
-            mv = small.tile([P, 2, 2], F32, name="mv")
-            for i in range(2):
-                nc.vector.bn_aggr(
-                    out=mv[:, i, :], in_=st[:, i].rearrange("p n s -> p (n s)")
-                )
-            mvs[s] = mv
+        def stats(s, n):
+            if n == 0:
+                sts[s] = small.tile([P, 2, 6], F32, name="st")
+            nc.vector.bn_stats(out=sts[s][:, n, :], in_=ys[(s, n)][:])
 
-        def affine_pair(s):
+        def aggr(s):
+            i = s % 2
+            if i == 0:
+                mvs[s] = small.tile([P, 2, 2], F32, name="mv")
+            nc.vector.bn_aggr(
+                out=mvs[s - i][:, i, :], in_=sts[s][:].rearrange("p n s -> p (n s)")
+            )
+
+        def stats_pair(s):
+            stats(s, 0)
+            if s % NT == 2 or s == 0:
+                pass
+            else:
+                aggr(s - 1)
+            stats(s, 1)
+            stats(s + 1, 0)
+            aggr(s)
+            stats(s + 1, 1)
+
+        def rstd_pair(s):
             mv = mvs[s]
-            ve = small.tile([P, 2], F32, name="ve")
-            nc.gpsimd.tensor_scalar(
-                out=ve[:], in0=mv[:, :, 1], scalar1=1.0, scalar2=EPS,
-                op0=ALU.mult, op1=ALU.add,
-            )
             rstd = small.tile([P, 2], F32, name="rstd")
-            nc.gpsimd.tensor_tensor(out=rstd[:], in0=ve[:], in1=mhalf[:], op=ALU.pow)
-            negmu = small.tile([P, 2], F32, name="negmu")
-            nc.gpsimd.tensor_scalar(
-                out=negmu[:], in0=mv[:, :, 0], scalar1=-1.0, scalar2=0.0,
-                op0=ALU.mult, op1=ALU.add,
+            nc.scalar.activation(
+                out=rstd[:], in_=mv[:, :, 1], func=ACT.Abs_reciprocal_sqrt, bias=epst[:, 0:1]
             )
+            negmu = small.tile([P, 2], F32, name="negmu")
+            nc.scalar.activation(out=negmu[:], in_=mv[:, :, 0], func=ACT.Identity, scale=-1.0)
+            aff[s] = (rstd, negmu)
+
+        def bias_pair(s):
+            rstd, negmu = aff[s]
             nbias = small.tile([P, 2], F32, name="nbias")
-            nc.gpsimd.tensor_tensor(out=nbias[:], in0=negmu[:], in1=rstd[:], op=ALU.mult)
+            for i in range(2):
+                nc.scalar.activation(
+                    out=nbias[:, i : i + 1], in_=negmu[:, i : i + 1], func=ACT.Identity,
+                    scale=rstd[:, i : i + 1],
+                )
             aff[s] = (rstd, nbias)
 
         def norm(s):
@@ -231,14 +257,10 @@ def tile_lingunet5filter_pa_kernel(tc, x2, l2fs, out):
         def v_prep(k):
             regroup(vcopy, k, CG, CV)
 
-        def g_piece(r):
-            k = r // 2
-            j = r % 2
-            regroup_g(k, j * CG // 2, (j + 1) * CG // 2)
-
         def quant_run(k):
             quant_f(k)
-            quant_x(k, 0, POS)
+            quant_x(k, CG, POS)
+            quant_x(k, 0, CG)
 
         load_f(0)
         load_x_half(0, 0)
@@ -259,8 +281,7 @@ def tile_lingunet5filter_pa_kernel(tc, x2, l2fs, out):
         regroup(vcopy, 0, BANK, BANK + CV0)
         regroup(scopy, 0, BANK + CV0, POS)
         quant_x(0, BANK, POS)
-        g_piece(2)
-        g_piece(3)
+        regroup_g(1, 0, CG)
         mm(pv, "yv", ys, 0)
         mm(pv, "yv", ys, 1)
         v_prep(1)
@@ -272,34 +293,43 @@ def tile_lingunet5filter_pa_kernel(tc, x2, l2fs, out):
                 fcopy(k, j)
             for j in range(2):
                 s_piece(k, j)
-        g_piece(4)
 
         for step in range(last + LAG):
-            if step < last:
-                if step % 2 == 0:
-                    stats_pair(step)
-                    if step % NT == 0 and step // NT + 1 < NB:
-                        quant_run(step // NT + 1)
-                    affine_pair(step)
-                    r = step // 2 + 5
-                    if r // 2 < NB:
-                        g_piece(r)
-                    if step % NT == 2 and (step + 6) // NT < NB:
-                        v_prep((step + 6) // NT)
+            if step == last:
+                aggr(last - 1)
+            if step < last and step % 2 == 0:
+                stats_pair(step)
+                k = step // NT + 1
+                if step % NT == 0:
+                    if k + 1 < NB:
+                        v_prep(k + 1)
+                    aggr(step + 1)
+                    if k < NB:
+                        quant_run(k)
+                    if k + 1 < NB:
+                        regroup_g(k + 1, 0, CG)
             s = step - LAG
-            if s >= 0:
-                k = s // NT + 3
-                slot = s % NT
-                mm(ps, "sbank", yn, s)
-                if k < NB and slot % 2 == 0:
-                    transposes(k, slot // 2)
-            if step + 2 < last:
-                mm(pv, "yv", ys, step + 2)
+            ahead = s + 1
+            chain = ahead >= 0 and ahead % 2 == 0 and ahead < last
+            if chain:
+                rstd_pair(ahead)
             if s >= 0:
                 norm(s)
                 store(s)
+            if chain:
+                bias_pair(ahead)
+            if s >= 0:
+                k = s // NT + 3
                 if k < NB:
-                    if slot % 2 == 0:
-                        fcopy(k, slot // 2)
+                    if s % 2 == 0:
+                        fcopy(k, s % NT // 2)
                     else:
-                        s_piece(k, slot // 2)
+                        s_piece(k, s % NT // 2)
+            n = step - LAG_P
+            if 0 <= n < last:
+                mm(ps, "sbank", yn, n)
+            ahead = step - LAG + 1
+            if ahead >= 0 and ahead % 2 == 0 and ahead // NT + 3 < NB:
+                transposes(ahead // NT + 3, ahead % NT // 2)
+            if step + 2 < last:
+                mm(pv, "yv", ys, step + 2)

@@ -20,9 +20,10 @@ BANK = 512
 EPS = 1e-5
 FLOPS = 2 * NB * CH * CH * POS
 CG = 512
-CV = 704
+CGG = 704
+CV = 832
 CV0 = 336
-VTAIL = 2
+VTAIL = 3
 FINE = 5
 LAG = 3
 LAG_P = 2
@@ -188,14 +189,14 @@ def tile_lingunet5filter_pa_kernel(tc, x2, l2fs, out):
 
         def stats_pair(s):
             stats(s, 0)
-            if s % NT == 2 or s == 0:
-                pass
-            else:
+            if s % NT == 0 and s > 0:
                 aggr(s - 1)
             stats(s, 1)
             stats(s + 1, 0)
             aggr(s)
             stats(s + 1, 1)
+            if s >= NB * NT - NT:
+                aggr(s + 1)
 
         def rstd_pair(s):
             mv = mvs[s]
@@ -217,29 +218,57 @@ def tile_lingunet5filter_pa_kernel(tc, x2, l2fs, out):
                 )
             aff[s] = (rstd, nbias)
 
-        def norm(s):
+        def chain_tile(s):
             i = s % 2
-            rstd, nbias = aff[s - i]
+            mv = mvs[s - i]
+            rstd = small.tile([P, 1], F32, name="rstd1")
+            nc.scalar.activation(
+                out=rstd[:], in_=mv[:, i, 1:2], func=ACT.Abs_reciprocal_sqrt, bias=epst[:, 0:1]
+            )
+            negmu = small.tile([P, 1], F32, name="negmu1")
+            nc.scalar.activation(out=negmu[:], in_=mv[:, i, 0:1], func=ACT.Identity, scale=-1.0)
+            nbias = small.tile([P, 1], F32, name="nbias1")
+            nc.scalar.activation(
+                out=nbias[:], in_=negmu[:], func=ACT.Identity, scale=rstd[:, 0:1]
+            )
+            return rstd, nbias
+
+        def norm(s, between):
+            i = s % 2
+            if s >= NB * NT - 2:
+                rstd, nbias = chain_tile(s)
+                j = 0
+            else:
+                rstd, nbias = aff[s - i]
+                j = i
             if i == 0:
                 osb[s // 2] = outp.tile([P, 2, POS], F32, name="osb")
             for n in range(2):
+                if n == 1 and between >= 0:
+                    rstd_pair(between)
                 dst = osb[s // 2][:, i, n * BANK : (n + 1) * BANK]
                 if n == 1 and s >= NB * NT - VTAIL:
                     nc.vector.tensor_scalar(
                         out=dst, in0=yn[(s, n)][:],
-                        scalar1=mvs[s - i][:, i, 0:1], scalar2=rstd[:, i : i + 1],
+                        scalar1=mvs[s - i][:, i, 0:1], scalar2=rstd[:, j : j + 1],
                         op0=ALU.subtract, op1=ALU.mult,
                     )
                 else:
                     nc.scalar.activation(
                         out=dst, in_=yn[(s, n)][:], func=ACT.Identity,
-                        bias=nbias[:, i : i + 1], scale=rstd[:, i : i + 1],
+                        bias=nbias[:, j : j + 1], scale=rstd[:, j : j + 1],
                     )
 
         def store(s):
             b = s // NT
             t = s % NT
-            if b >= FINE:
+            if s >= NB * NT - 2:
+                for n in range(2):
+                    cols = slice(n * BANK, (n + 1) * BANK)
+                    nc.sync.dma_start(
+                        out=ov[b][:, t : t + 1, cols], in_=osb[s // 2][:, t % 2 : t % 2 + 1, cols]
+                    )
+            elif b >= FINE:
                 nc.sync.dma_start(
                     out=ov[b][:, t : t + 1, :], in_=osb[s // 2][:, t % 2 : t % 2 + 1, :]
                 )
@@ -254,13 +283,12 @@ def tile_lingunet5filter_pa_kernel(tc, x2, l2fs, out):
         def s_piece(k, j):
             regroup(scopy, k, (CV, mid_s)[j], (mid_s, POS)[j])
 
-        def v_prep(k):
-            regroup(vcopy, k, CG, CV)
+        def g_prep(k):
+            regroup_g(k, 0, CG)
+            regroup_g(k, CG, CGG)
 
-        def quant_run(k):
-            quant_f(k)
-            quant_x(k, CG, POS)
-            quant_x(k, 0, CG)
+        def v_prep(k):
+            regroup(vcopy, k, CGG, CV)
 
         load_f(0)
         load_x_half(0, 0)
@@ -281,10 +309,9 @@ def tile_lingunet5filter_pa_kernel(tc, x2, l2fs, out):
         regroup(vcopy, 0, BANK, BANK + CV0)
         regroup(scopy, 0, BANK + CV0, POS)
         quant_x(0, BANK, POS)
-        regroup_g(1, 0, CG)
+        g_prep(1)
         mm(pv, "yv", ys, 0)
         mm(pv, "yv", ys, 1)
-        v_prep(1)
         for k in range(1, 3):
             if k == 2:
                 for j in range(2):
@@ -294,28 +321,30 @@ def tile_lingunet5filter_pa_kernel(tc, x2, l2fs, out):
             for j in range(2):
                 s_piece(k, j)
 
+        v_prep(1)
+        nn = 0
         for step in range(last + LAG):
-            if step == last:
-                aggr(last - 1)
             if step < last and step % 2 == 0:
                 stats_pair(step)
                 k = step // NT + 1
                 if step % NT == 0:
-                    if k + 1 < NB:
-                        v_prep(k + 1)
-                    aggr(step + 1)
                     if k < NB:
-                        quant_run(k)
+                        quant_f(k)
+                        aggr(step + 1)
+                        if k + 1 < NB:
+                            v_prep(k + 1)
+                        quant_x(k, CG, POS)
+                        quant_x(k, 0, CG)
                     if k + 1 < NB:
-                        regroup_g(k + 1, 0, CG)
+                        g_prep(k + 1)
             s = step - LAG
             ahead = s + 1
-            chain = ahead >= 0 and ahead % 2 == 0 and ahead < last
-            if chain:
-                rstd_pair(ahead)
+            chain = ahead >= 0 and ahead % 2 == 0 and ahead < last - 2
             if s >= 0:
-                norm(s)
+                norm(s, ahead if chain else -1)
                 store(s)
+            elif chain:
+                rstd_pair(ahead)
             if chain:
                 bias_pair(ahead)
             if s >= 0:
@@ -325,9 +354,9 @@ def tile_lingunet5filter_pa_kernel(tc, x2, l2fs, out):
                         fcopy(k, s % NT // 2)
                     else:
                         s_piece(k, s % NT // 2)
-            n = step - LAG_P
-            if 0 <= n < last:
-                mm(ps, "sbank", yn, n)
+            while nn < last and nn <= step - (LAG_P if step < last - NT else 1):
+                mm(ps, "sbank", yn, nn)
+                nn += 1
             ahead = step - LAG + 1
             if ahead >= 0 and ahead % 2 == 0 and ahead // NT + 3 < NB:
                 transposes(ahead // NT + 3, ahead % NT // 2)

@@ -31,8 +31,8 @@ LAG_P = 2
 
 def tile_lingunet5filter_pa_kernel(tc, x2, l2fs, out):
     nc = tc.nc
-    xv = x2.rearrange("b (u p e) h w -> b p u (e h w)", u=2, e=2)
-    xh = x2.rearrange("b (u p e) h w -> b u p e (h w)", u=2, e=2)
+    xv = x2.rearrange("b (p t) h w -> b p (t h w)", t=4)
+    xh = x2.rearrange("b (p t) h w -> b p t (h w)", t=4)
     fv = l2fs.rearrange("b (p t) k x y -> b p (t k x y)", t=NT)
     ov = out.rearrange("b (p t) h w -> b p t (h w)", t=NT)
 
@@ -78,17 +78,14 @@ def tile_lingunet5filter_pa_kernel(tc, x2, l2fs, out):
         def load_x(b):
             xraw[b] = raw.tile([P, 4, POS], BF16, name="xraw")
             nc.sync.dma_start(
-                out=xraw[b][:].rearrange("p (u e) w -> p u (e w)", u=2), in_=xv[b]
+                out=xraw[b][:].rearrange("p t w -> p (t w)"), in_=xv[b]
             )
 
         def load_x_half(b, h):
             if b not in xraw:
                 xraw[b] = raw.tile([P, 4, POS], BF16, name="xraw")
-            for u in range(2):
-                nc.sync.dma_start(
-                    out=xraw[b][:, 2 * u : 2 * u + 2, h * BANK : (h + 1) * BANK],
-                    in_=xh[b][u][:, :, h * BANK : (h + 1) * BANK],
-                )
+            cols = slice(h * BANK, (h + 1) * BANK)
+            nc.sync.dma_start(out=xraw[b][:, :, cols], in_=xh[b][:, :, cols])
 
         def load_f(b):
             fraw[b] = raw.tile([P, NT * CH], BF16, name="fraw")
@@ -99,9 +96,9 @@ def tile_lingunet5filter_pa_kernel(tc, x2, l2fs, out):
             ft[(b, j)] = ps.tile([P, 2, 2, P], F32, name="ft", tag="sbank")
             for tt in range(2):
                 for u in range(2):
-                    c0 = (2 * j + tt) * 256 + u * P
+                    c0 = (2 * j + tt) * 256
                     nc.tensor.transpose(
-                        ft[(b, j)][:, tt, u, :], fw[:, c0 : c0 + P], ident[:]
+                        ft[(b, j)][:, tt, u, :], fw[:, c0 + u : c0 + 2 * P : 2], ident[:]
                     )
 
         def fcopy(b, j):

@@ -20,8 +20,8 @@ BANK = 512
 EPS = 1e-5
 FLOPS = 2 * NB * CH * CH * POS
 CG = 512
-CGG = 704
-CV = 832
+CGG = 672
+CV = 768
 CV0 = 336
 VTAIL = 3
 FINE = 5
@@ -58,6 +58,9 @@ def tile_lingunet5filter_pa_kernel(tc, x2, l2fs, out):
         )
         warm = const.tile([P, 2], F32, name="warm")
         nc.scalar.activation(out=warm[:], in_=mhalf[:], func=ACT.Abs_reciprocal_sqrt)
+
+        dummy = const.tile([P, BANK], BF16, name="dummy")
+        nc.vector.memset(dummy[:], 0.0)
 
         ctx.enter_context(tc.manual_schedule())
 
@@ -294,9 +297,13 @@ def tile_lingunet5filter_pa_kernel(tc, x2, l2fs, out):
             load_f(b)
             load_x(b)
 
-        for b in range(2):
-            for j in range(2):
-                transposes(b, j)
+        for j in range(2):
+            transposes(0, j)
+        junk = pv.tile([P, BANK], F32, name="junk", tag="yv")
+        for i in range(3):
+            nc.tensor.matmul(junk[:], dummy[:, 0:P], dummy[:], start=True, stop=True)
+        for j in range(2):
+            transposes(1, j)
         fcopy(0, 0)
         fcopy(0, 1)
         regroup(vcopy, 0, 0, CV0)
@@ -306,7 +313,7 @@ def tile_lingunet5filter_pa_kernel(tc, x2, l2fs, out):
         regroup(vcopy, 0, BANK, BANK + CV0)
         regroup(scopy, 0, BANK + CV0, POS)
         quant_x(0, BANK, POS)
-        g_prep(1)
+        regroup_g(1, 0, 384)
         mm(pv, "yv", ys, 0)
         mm(pv, "yv", ys, 1)
         for k in range(1, 3):
@@ -317,17 +324,23 @@ def tile_lingunet5filter_pa_kernel(tc, x2, l2fs, out):
                 fcopy(k, j)
             for j in range(2):
                 s_piece(k, j)
+            if k == 1:
+                regroup(scopy, 1, CG, CGG)
 
-        v_prep(1)
         nn = 0
         for step in range(last + LAG):
             if step < last and step % 2 == 0:
                 stats_pair(step)
+                if step == 0:
+                    aggr(1)
+                    regroup(vcopy, 1, 384, CG)
+                    v_prep(1)
                 k = step // NT + 1
                 if step % NT == 0:
                     if k < NB:
                         quant_f(k)
-                        aggr(step + 1)
+                        if step > 0:
+                            aggr(step + 1)
                         if k + 1 < NB:
                             v_prep(k + 1)
                         quant_x(k, CG, POS)
@@ -351,7 +364,7 @@ def tile_lingunet5filter_pa_kernel(tc, x2, l2fs, out):
                         fcopy(k, s % NT // 2)
                     else:
                         s_piece(k, s % NT // 2)
-            while nn < last and nn <= step - (LAG_P if step < last - NT else 1):
+            while nn < last and nn <= step - (LAG_P if 4 <= step < last - NT else 1):
                 mm(ps, "sbank", yn, nn)
                 nn += 1
             ahead = step - LAG + 1

@@ -22,9 +22,9 @@ FLOPS = 2 * NB * CH * CH * POS
 CG = 512
 CGG = 672
 CV = 768
-CV0 = 336
+CV0 = 272
 VTAIL = 3
-FINE = 5
+FINE = 4
 LAG = 3
 LAG_P = 2
 
@@ -198,71 +198,50 @@ def tile_lingunet5filter_pa_kernel(tc, x2, l2fs, out):
             if s >= NB * NT - NT:
                 aggr(s + 1)
 
-        def rstd_pair(s):
-            mv = mvs[s]
-            rstd = small.tile([P, 2], F32, name="rstd")
+        def rstd_of(s, w):
+            i = s % 2
+            mv = mvs[s - i]
+            rstd = small.tile([P, w], F32, name="rstd")
             nc.scalar.activation(
-                out=rstd[:], in_=mv[:, :, 1], func=ACT.Abs_reciprocal_sqrt, bias=epst[:, 0:1]
+                out=rstd[:], in_=mv[:, i : i + w, 1], func=ACT.Abs_reciprocal_sqrt,
+                bias=epst[:, 0:1],
             )
-            negmu = small.tile([P, 2], F32, name="negmu")
-            nc.scalar.activation(out=negmu[:], in_=mv[:, :, 0], func=ACT.Identity, scale=-1.0)
+            negmu = small.tile([P, w], F32, name="negmu")
+            nc.scalar.activation(
+                out=negmu[:], in_=mv[:, i : i + w, 0], func=ACT.Identity, scale=-1.0
+            )
             aff[s] = (rstd, negmu)
 
-        def bias_pair(s):
+        def bias_of(s, w):
             rstd, negmu = aff[s]
-            nbias = small.tile([P, 2], F32, name="nbias")
-            for i in range(2):
+            nbias = small.tile([P, w], F32, name="nbias")
+            for i in range(w):
                 nc.scalar.activation(
                     out=nbias[:, i : i + 1], in_=negmu[:, i : i + 1], func=ACT.Identity,
                     scale=rstd[:, i : i + 1],
                 )
-            aff[s] = (rstd, nbias)
+                aff[s + i] = (rstd[:, i : i + 1], nbias[:, i : i + 1])
 
-        def chain_tile(s):
+        def norm(s, n):
             i = s % 2
-            mv = mvs[s - i]
-            rstd = small.tile([P, 1], F32, name="rstd1")
-            nc.scalar.activation(
-                out=rstd[:], in_=mv[:, i, 1:2], func=ACT.Abs_reciprocal_sqrt, bias=epst[:, 0:1]
-            )
-            negmu = small.tile([P, 1], F32, name="negmu1")
-            nc.scalar.activation(out=negmu[:], in_=mv[:, i, 0:1], func=ACT.Identity, scale=-1.0)
-            nbias = small.tile([P, 1], F32, name="nbias1")
-            nc.scalar.activation(
-                out=nbias[:], in_=negmu[:], func=ACT.Identity, scale=rstd[:, 0:1]
-            )
-            return rstd, nbias
-
-        def norm(s, between):
-            i = s % 2
-            if s >= NB * NT - 2:
-                rstd, nbias = chain_tile(s)
-                j = 0
-            else:
-                rstd, nbias = aff[s - i]
-                j = i
-            if i == 0:
+            if i == 0 and n == 0:
                 osb[s // 2] = outp.tile([P, 2, POS], F32, name="osb")
-            for n in range(2):
-                if n == 1 and between >= 0:
-                    rstd_pair(between)
-                dst = osb[s // 2][:, i, n * BANK : (n + 1) * BANK]
-                if n == 1 and s >= NB * NT - VTAIL:
-                    nc.vector.tensor_scalar(
-                        out=dst, in0=yn[(s, n)][:],
-                        scalar1=mvs[s - i][:, i, 0:1], scalar2=rstd[:, j : j + 1],
-                        op0=ALU.subtract, op1=ALU.mult,
-                    )
-                else:
-                    nc.scalar.activation(
-                        out=dst, in_=yn[(s, n)][:], func=ACT.Identity,
-                        bias=nbias[:, j : j + 1], scale=rstd[:, j : j + 1],
-                    )
+            dst = osb[s // 2][:, i, n * BANK : (n + 1) * BANK]
+            rstd, nbias = aff[s]
+            if n == 1 and s >= NB * NT - VTAIL:
+                nc.vector.tensor_scalar(
+                    out=dst, in0=yn[(s, n)][:], scalar1=mvs[s - i][:, i, 0:1], scalar2=rstd,
+                    op0=ALU.subtract, op1=ALU.mult,
+                )
+            else:
+                nc.scalar.activation(
+                    out=dst, in_=yn[(s, n)][:], func=ACT.Identity, bias=nbias, scale=rstd
+                )
 
         def store(s):
             b = s // NT
             t = s % NT
-            if s >= NB * NT - 2:
+            if s >= NB * NT - 4:
                 for n in range(2):
                     cols = slice(n * BANK, (n + 1) * BANK)
                     nc.sync.dma_start(
@@ -290,7 +269,10 @@ def tile_lingunet5filter_pa_kernel(tc, x2, l2fs, out):
         def v_prep(k):
             regroup(vcopy, k, CGG, CV)
 
-        load_f(0)
+        fraw[0] = raw.tile([P, NT * CH], BF16, name="fraw")
+        for j in range(2):
+            cols = slice(j * 2 * CH, (j + 1) * 2 * CH)
+            nc.sync.dma_start(out=fraw[0][:, cols], in_=fv[0][:, cols])
         load_x_half(0, 0)
         load_x_half(0, 1)
         for b in range(1, NB):
@@ -306,9 +288,9 @@ def tile_lingunet5filter_pa_kernel(tc, x2, l2fs, out):
             transposes(1, j)
         fcopy(0, 0)
         fcopy(0, 1)
+        quant_f(0)
         regroup(vcopy, 0, 0, CV0)
         regroup(scopy, 0, CV0, BANK)
-        quant_f(0)
         quant_x(0, 0, BANK)
         regroup(vcopy, 0, BANK, BANK + CV0)
         regroup(scopy, 0, BANK + CV0, POS)
@@ -351,12 +333,21 @@ def tile_lingunet5filter_pa_kernel(tc, x2, l2fs, out):
             ahead = s + 1
             chain = ahead >= 0 and ahead % 2 == 0 and ahead < last - 2
             if s >= 0:
-                norm(s, ahead if chain else -1)
-                store(s)
-            elif chain:
-                rstd_pair(ahead)
+                norm(s, 0)
             if chain:
-                bias_pair(ahead)
+                rstd_of(ahead, 2)
+            if s == last - 4:
+                rstd_of(last - 2, 1)
+            if s == last - 3:
+                bias_of(last - 1, 1)
+            if s >= 0:
+                norm(s, 1)
+                store(s)
+            if chain:
+                bias_of(ahead, 2)
+            if s == last - 4:
+                bias_of(last - 2, 1)
+                rstd_of(last - 1, 1)
             if s >= 0:
                 k = s // NT + 3
                 if k < NB:
@@ -364,8 +355,11 @@ def tile_lingunet5filter_pa_kernel(tc, x2, l2fs, out):
                         fcopy(k, s % NT // 2)
                     else:
                         s_piece(k, s % NT // 2)
-            while nn < last and nn <= step - (LAG_P if 4 <= step < last - NT else 1):
-                mm(ps, "sbank", yn, nn)
+            while nn < last and nn <= step - (LAG_P if 4 <= step < last - 2 * NT else 1):
+                if nn < last - 2:
+                    mm(ps, "sbank", yn, nn)
+                else:
+                    mm(pv, "yv", yn, nn)
                 nn += 1
             ahead = step - LAG + 1
             if ahead >= 0 and ahead % 2 == 0 and ahead // NT + 3 < NB:

@@ -21,7 +21,7 @@ EPS = 1e-5
 FLOPS = 2 * NB * CH * CH * POS
 CG = 512
 CGG = 672
-CV = 768
+CV = 736
 CV0 = 272
 VTAIL = 3
 FINE = 4
@@ -189,13 +189,13 @@ def tile_lingunet5filter_pa_kernel(tc, x2, l2fs, out):
 
         def stats_pair(s):
             stats(s, 0)
-            if s % NT == 0 and s > 0:
+            if s % NT == 0 and s > 0 or s == NB * NT - 2:
                 aggr(s - 1)
             stats(s, 1)
             stats(s + 1, 0)
             aggr(s)
             stats(s + 1, 1)
-            if s >= NB * NT - NT:
+            if s == NB * NT - 2:
                 aggr(s + 1)
 
         def rstd_of(s, w):
@@ -291,9 +291,9 @@ def tile_lingunet5filter_pa_kernel(tc, x2, l2fs, out):
         quant_f(0)
         regroup(vcopy, 0, 0, CV0)
         regroup(scopy, 0, CV0, BANK)
-        quant_x(0, 0, BANK)
         regroup(vcopy, 0, BANK, BANK + CV0)
         regroup(scopy, 0, BANK + CV0, POS)
+        quant_x(0, 0, BANK)
         quant_x(0, BANK, POS)
         regroup_g(1, 0, 384)
         mm(pv, "yv", ys, 0)
@@ -314,8 +314,8 @@ def tile_lingunet5filter_pa_kernel(tc, x2, l2fs, out):
             if step < last and step % 2 == 0:
                 stats_pair(step)
                 if step == 0:
-                    aggr(1)
                     regroup(vcopy, 1, 384, CG)
+                    aggr(1)
                     v_prep(1)
                 k = step // NT + 1
                 if step % NT == 0:

from contextlib import ExitStack

import concourse.mybir as mybir
from concourse.masks import make_identity

F32 = mybir.dt.float32
BF16 = mybir.dt.bfloat16
U32 = mybir.dt.uint32
U8 = mybir.dt.uint8
FP8X4 = mybir.dt.float8_e4m3fn_x4
ACT = mybir.ActivationFunctionType
ALU = mybir.AluOpType

NB = 8
CH = 512
POS = 1024
P = 128
NT = 4
BANK = 512
EPS = 1e-5
FLOPS = 2 * NB * CH * CH * POS
CG = 512
CGG = 672
CV = 736
CV0 = 272
VTAIL = 3
FINE = 4
LAG = 3
LAG_P = 2


def tile_lingunet5filter_pa_kernel(tc, x2, l2fs, out):
    nc = tc.nc
    xv = x2.rearrange("b (p t) h w -> b p (t h w)", t=4)
    xh = x2.rearrange("b (p t) h w -> b p t (h w)", t=4)
    fv = l2fs.rearrange("b (p t) k x y -> b p (t k x y)", t=NT)
    ov = out.rearrange("b (p t) h w -> b p t (h w)", t=NT)

    with ExitStack() as ctx:
        const = ctx.enter_context(tc.tile_pool(name="const", bufs=1))
        raw = ctx.enter_context(tc.tile_pool(name="raw", bufs=NB))
        gone = ctx.enter_context(tc.tile_pool(name="gone", bufs=1))
        grp = ctx.enter_context(tc.tile_pool(name="grp", bufs=3))
        mxp = ctx.enter_context(tc.tile_pool(name="mxp", bufs=3))
        outp = ctx.enter_context(tc.tile_pool(name="outp", bufs=8))
        small = ctx.enter_context(tc.tile_pool(name="small", bufs=8))
        pv = ctx.enter_context(tc.psum_pool(name="pv", bufs=4))
        ps = ctx.enter_context(tc.psum_pool(name="ps", bufs=4))

        ident = const.tile([P, P], F32, name="ident")
        make_identity(nc, ident[:])
        mhalf = const.tile([P, 2], F32, name="mhalf")
        nc.vector.memset(mhalf[:], -0.5)
        epst = const.tile([P, 1], F32, name="epst")
        nc.vector.tensor_scalar(
            out=epst[:], in0=mhalf[:, 0:1], scalar1=0.0, scalar2=EPS,
            op0=ALU.mult, op1=ALU.add,
        )
        warm = const.tile([P, 2], F32, name="warm")
        nc.scalar.activation(out=warm[:], in_=mhalf[:], func=ACT.Abs_reciprocal_sqrt)

        dummy = const.tile([P, BANK], BF16, name="dummy")
        nc.vector.memset(dummy[:], 0.0)

        ctx.enter_context(tc.manual_schedule())

        xraw = {}
        fraw = {}
        xg = {}
        fg = {}
        ft = {}
        xq = {}
        fq = {}
        ys = {}
        yn = {}
        sts = {}
        mvs = {}
        aff = {}
        osb = {}

        def load_x(b):
            xraw[b] = raw.tile([P, 4, POS], BF16, name="xraw")
            nc.sync.dma_start(
                out=xraw[b][:].rearrange("p t w -> p (t w)"), in_=xv[b]
            )

        def load_x_half(b, h):
            if b not in xraw:
                xraw[b] = raw.tile([P, 4, POS], BF16, name="xraw")
            cols = slice(h * BANK, (h + 1) * BANK)
            nc.sync.dma_start(out=xraw[b][:, :, cols], in_=xh[b][:, :, cols])

        def load_f(b):
            fraw[b] = raw.tile([P, NT * CH], BF16, name="fraw")
            nc.sync.dma_start(out=fraw[b][:], in_=fv[b])

        def transposes(b, j):
            fw = fraw[b][:].bitcast(F32)
            ft[(b, j)] = ps.tile([P, 2, 2, P], F32, name="ft", tag="sbank")
            for tt in range(2):
                for u in range(2):
                    c0 = (2 * j + tt) * 256
                    nc.tensor.transpose(
                        ft[(b, j)][:, tt, u, :], fw[:, c0 + u : c0 + 2 * P : 2], ident[:]
                    )

        def fcopy(b, j):
            if b not in fg:
                fg[b] = grp.tile([P, 4 * CH], BF16, name="fg", align_bytes=64)
            fgw = fg[b][:].bitcast(F32).rearrange(
                "p (j tt o u) -> p j tt o u", j=2, tt=2, u=2
            )
            nc.scalar.copy(
                out=fgw[:, j], in_=ft[(b, j)][:].rearrange("p tt u o -> p tt o u")
            )

        def grouped(b, c0, c1):
            if c1 <= CG:
                if (b, 0) not in xg:
                    xg[(b, 0)] = gone.tile([P, 4 * CG], BF16, name="xga", align_bytes=64)
                return xg[(b, 0)][:, 4 * c0 : 4 * c1]
            if (b, 1) not in xg:
                xg[(b, 1)] = grp.tile([P, 4 * (POS - CG)], BF16, name="xgb", align_bytes=64)
            return xg[(b, 1)][:, 4 * (c0 - CG) : 4 * (c1 - CG)]

        def regroup(copy, b, c0, c1):
            copy(
                out=grouped(b, c0, c1).rearrange("p (c i t) -> p c t i", i=4, t=4),
                in_=xraw[b][:, :, c0:c1].rearrange("p t (c i) -> p c t i", i=4),
            )

        def regroup_g(b, c0, c1):
            nc.gpsimd.tensor_scalar(
                out=grouped(b, c0, c1).rearrange("p (c t) -> p c t", t=4),
                in0=xraw[b][:, :, c0:c1].rearrange("p t c -> p c t"),
                scalar1=1.0, scalar2=0.0, op0=ALU.mult, op1=ALU.add,
            )

        def quant_f(b):
            codes = mxp.tile([P, CH], U32, name="fc", align_bytes=64)
            scales = mxp.tile([P, CH], U8, name="fs", align_bytes=64)
            nc.vector.quantize_mx(
                out=codes[:].bitcast(FP8X4), scales=scales[:], in_=fg[b][:]
            )
            fq[b] = (codes, scales)

        def quant_x(b, c0, c1):
            if b not in xq:
                codes = mxp.tile([P, POS], U32, name="xc", align_bytes=64)
                scales = mxp.tile([P, POS], U8, name="xs", align_bytes=64)
                xq[b] = (codes, scales)
            codes, scales = xq[b]
            nc.vector.quantize_mx(
                out=codes[:, c0:c1].bitcast(FP8X4),
                scales=scales[:, c0:c1],
                in_=grouped(b, c0, c1),
            )

        def mm(pool, tag, keep, s):
            b = s // NT
            t = s % NT
            fc, fs = fq[b]
            xc, xs = xq[b]
            for n in range(2):
                y = pool.tile([P, BANK], F32, name=tag)
                nc.tensor.matmul_mx(
                    out=y[:],
                    lhsT=fc[:, t * P : (t + 1) * P].bitcast(FP8X4),
                    lhsT_scale=fs[:, t * P : (t + 1) * P],
                    rhs=xc[:, n * BANK : (n + 1) * BANK].bitcast(FP8X4),
                    rhs_scale=xs[:, n * BANK : (n + 1) * BANK],
                    start=True,
                    stop=True,
                )
                keep[(s, n)] = y

        def stats(s, n):
            if n == 0:
                sts[s] = small.tile([P, 2, 6], F32, name="st")
            nc.vector.bn_stats(out=sts[s][:, n, :], in_=ys[(s, n)][:])

        def aggr(s):
            i = s % 2
            if i == 0:
                mvs[s] = small.tile([P, 2, 2], F32, name="mv")
            nc.vector.bn_aggr(
                out=mvs[s - i][:, i, :], in_=sts[s][:].rearrange("p n s -> p (n s)")
            )

        def stats_pair(s):
            stats(s, 0)
            if s % NT == 0 and s > 0 or s == NB * NT - 2:
                aggr(s - 1)
            stats(s, 1)
            stats(s + 1, 0)
            aggr(s)
            stats(s + 1, 1)
            if s == NB * NT - 2:
                aggr(s + 1)

        def rstd_of(s, w):
            i = s % 2
            mv = mvs[s - i]
            rstd = small.tile([P, w], F32, name="rstd")
            nc.scalar.activation(
                out=rstd[:], in_=mv[:, i : i + w, 1], func=ACT.Abs_reciprocal_sqrt,
                bias=epst[:, 0:1],
            )
            negmu = small.tile([P, w], F32, name="negmu")
            nc.scalar.activation(
                out=negmu[:], in_=mv[:, i : i + w, 0], func=ACT.Identity, scale=-1.0
            )
            aff[s] = (rstd, negmu)

        def bias_of(s, w):
            rstd, negmu = aff[s]
            nbias = small.tile([P, w], F32, name="nbias")
            for i in range(w):
                nc.scalar.activation(
                    out=nbias[:, i : i + 1], in_=negmu[:, i : i + 1], func=ACT.Identity,
                    scale=rstd[:, i : i + 1],
                )
                aff[s + i] = (rstd[:, i : i + 1], nbias[:, i : i + 1])

        def norm(s, n):
            i = s % 2
            if i == 0 and n == 0:
                osb[s // 2] = outp.tile([P, 2, POS], F32, name="osb")
            dst = osb[s // 2][:, i, n * BANK : (n + 1) * BANK]
            rstd, nbias = aff[s]
            if n == 1 and s >= NB * NT - VTAIL:
                nc.vector.tensor_scalar(
                    out=dst, in0=yn[(s, n)][:], scalar1=mvs[s - i][:, i, 0:1], scalar2=rstd,
                    op0=ALU.subtract, op1=ALU.mult,
                )
            else:
                nc.scalar.activation(
                    out=dst, in_=yn[(s, n)][:], func=ACT.Identity, bias=nbias, scale=rstd
                )

        def store(s):
            b = s // NT
            t = s % NT
            if s >= NB * NT - 4:
                for n in range(2):
                    cols = slice(n * BANK, (n + 1) * BANK)
                    nc.sync.dma_start(
                        out=ov[b][:, t : t + 1, cols], in_=osb[s // 2][:, t % 2 : t % 2 + 1, cols]
                    )
            elif b >= FINE:
                nc.sync.dma_start(
                    out=ov[b][:, t : t + 1, :], in_=osb[s // 2][:, t % 2 : t % 2 + 1, :]
                )
            elif t % 2 == 1:
                nc.sync.dma_start(out=ov[b][:, t - 1 : t + 1, :], in_=osb[s // 2][:])

        vcopy = nc.vector.tensor_copy
        scopy = nc.scalar.copy
        mid_s = (CV + POS) // 2
        last = NB * NT

        def s_piece(k, j):
            regroup(scopy, k, (CV, mid_s)[j], (mid_s, POS)[j])

        def g_prep(k):
            regroup_g(k, 0, CG)
            regroup_g(k, CG, CGG)

        def v_prep(k):
            regroup(vcopy, k, CGG, CV)

        fraw[0] = raw.tile([P, NT * CH], BF16, name="fraw")
        for j in range(2):
            cols = slice(j * 2 * CH, (j + 1) * 2 * CH)
            nc.sync.dma_start(out=fraw[0][:, cols], in_=fv[0][:, cols])
        load_x_half(0, 0)
        load_x_half(0, 1)
        for b in range(1, NB):
            load_f(b)
            load_x(b)

        for j in range(2):
            transposes(0, j)
        junk = pv.tile([P, BANK], F32, name="junk", tag="yv")
        for i in range(3):
            nc.tensor.matmul(junk[:], dummy[:, 0:P], dummy[:], start=True, stop=True)
        for j in range(2):
            transposes(1, j)
        fcopy(0, 0)
        fcopy(0, 1)
        quant_f(0)
        regroup(vcopy, 0, 0, CV0)
        regroup(scopy, 0, CV0, BANK)
        regroup(vcopy, 0, BANK, BANK + CV0)
        regroup(scopy, 0, BANK + CV0, POS)
        quant_x(0, 0, BANK)
        quant_x(0, BANK, POS)
        regroup_g(1, 0, 384)
        mm(pv, "yv", ys, 0)
        mm(pv, "yv", ys, 1)
        for k in range(1, 3):
            if k == 2:
                for j in range(2):
                    transposes(k, j)
            for j in range(2):
                fcopy(k, j)
            for j in range(2):
                s_piece(k, j)
            if k == 1:
                regroup(scopy, 1, CG, CGG)

        nn = 0
        for step in range(last + LAG):
            if step < last and step % 2 == 0:
                stats_pair(step)
                if step == 0:
                    regroup(vcopy, 1, 384, CG)
                    aggr(1)
                    v_prep(1)
                k = step // NT + 1
                if step % NT == 0:
                    if k < NB:
                        quant_f(k)
                        if step > 0:
                            aggr(step + 1)
                        if k + 1 < NB:
                            v_prep(k + 1)
                        quant_x(k, CG, POS)
                        quant_x(k, 0, CG)
                    if k + 1 < NB:
                        g_prep(k + 1)
            s = step - LAG
            ahead = s + 1
            chain = ahead >= 0 and ahead % 2 == 0 and ahead < last - 2
            if s >= 0:
                norm(s, 0)
            if chain:
                rstd_of(ahead, 2)
            if s == last - 4:
                rstd_of(last - 2, 1)
            if s == last - 3:
                bias_of(last - 1, 1)
            if s >= 0:
                norm(s, 1)
                store(s)
            if chain:
                bias_of(ahead, 2)
            if s == last - 4:
                bias_of(last - 2, 1)
                rstd_of(last - 1, 1)
            if s >= 0:
                k = s // NT + 3
                if k < NB:
                    if s % 2 == 0:
                        fcopy(k, s % NT // 2)
                    else:
                        s_piece(k, s % NT // 2)
            while nn < last and nn <= step - (LAG_P if 4 <= step < last - 2 * NT else 1):
                if nn < last - 2:
                    mm(ps, "sbank", yn, nn)
                else:
                    mm(pv, "yv", yn, nn)
                nn += 1
            ahead = step - LAG + 1
            if ahead >= 0 and ahead % 2 == 0 and ahead // NT + 3 < NB:
                transposes(ahead // NT + 3, ahead % NT // 2)
            if step + 2 < last:
                mm(pv, "yv", ys, step + 2)
